import numpy as np
import ml_dtypes


def mxq(x, axis, fmt="e4m3"):
    dtype, down = {"e4m3": (ml_dtypes.float8_e4m3fn, 7), "e5m2": (ml_dtypes.float8_e5m2, 14)}[fmt]
    v = np.moveaxis(np.asarray(x, np.float32).astype(ml_dtypes.bfloat16).astype(np.float64), axis, -1)
    blocks = v.reshape(v.shape[:-1] + (-1, 32))
    amax = np.abs(blocks).max(-1, keepdims=True)
    byte = np.maximum(np.where(amax > 0, np.frexp(amax)[1] - 1 + 127, 0) - down, 1)
    scale = np.exp2(byte - 127.0)
    codes = (blocks / scale).astype(np.float32).astype(dtype).astype(np.float64)
    return np.moveaxis((codes * scale).reshape(v.shape), -1, axis)


WIDE = False


def mx_kscale(k):
    if not WIDE:
        return np.ones(k)
    levels = np.array([10, -10, 5, -5, 0])
    if k % 512:
        return np.exp2(np.random.permutation(np.resize(levels, k // 32))).repeat(32)
    a = np.empty((k // 512, 16))
    for p in range(k // 512):
        a[p, :8] = np.random.permutation(np.resize(levels, 8))
        for g in range(8):
            far = levels[np.abs(levels - a[p, g]) >= 10]
            a[p, g + 8] = far[np.random.randint(len(far))]
    return np.exp2(a.ravel()).repeat(32)


BF16 = ml_dtypes.bfloat16


def bf(x):
    return np.asarray(x, np.float32).astype(BF16)


def f64(x):
    return np.asarray(x).astype(np.float64)


B, S, H, NQ, NKV, HD, ROT = 2, 512, 1536, 12, 4, 128, 96
BASE = 10000.0


def rope(x):
    inv_freq = 1.0 / BASE ** (np.arange(0, ROT, 2) / ROT)
    freq = np.arange(S)[:, None] * inv_freq[None, :]
    emb = np.concatenate([freq, freq], axis=-1)
    cos = np.cos(emb)[None, :, None, :]
    sin = np.sin(emb)[None, :, None, :]
    x1, x2 = np.split(x, 2, axis=-1)
    half_rot = np.concatenate([-x2, x1], axis=-1)
    return x * cos + half_rot * sin


def draw0():
    s = mx_kscale(H)
    return {"hidden_states": bf(np.random.standard_normal((B, S, H)) * s),
            "Wq": bf(np.random.standard_normal((H, NQ, HD)) * 1.25 / np.sqrt(H) / s[:, None, None]),
            "Wk": bf(np.random.standard_normal((H, NKV, HD)) * 1.25 / np.sqrt(H) / s[:, None, None]),
            "Wv": bf(np.random.standard_normal((H, NKV, HD)) / np.sqrt(H) / s[:, None, None])}


def core(hidden_states, Wq, Wk, Wv):
    xq = mxq(f64(hidden_states), 2, "e4m3")
    q = (xq @ mxq(f64(Wq).reshape(H, NQ * HD), 0, "e4m3")).reshape(B, S, NQ, HD)
    k = (xq @ mxq(f64(Wk).reshape(H, NKV * HD), 0, "e4m3")).reshape(B, S, NKV, HD)
    v = (xq @ mxq(f64(Wv).reshape(H, NKV * HD), 0, "e4m3")).reshape(B, S, NKV, HD)
    q = np.concatenate([rope(q[..., :ROT]), q[..., ROT:]], axis=-1)
    k = np.concatenate([rope(k[..., :ROT]), k[..., ROT:]], axis=-1)
    return q, k, v


def e4m3fn_bytes(y):
    return np.clip(np.asarray(y, np.float64), -448.0, 448.0).astype(np.float32).astype(ml_dtypes.float8_e4m3fn).view(np.uint8)


def e4m3fn_values(b):
    return np.asarray(b, np.uint8).view(ml_dtypes.float8_e4m3fn).astype(np.float64)


def setup_inputs():
    d = draw0()
    x0 = np.asarray(d['Wq']).astype(np.float64)
    s = (np.max(np.abs(x0), axis=(1, 2), keepdims=True) / 448.0).astype(np.float32)
    out = {}
    for k, v in d.items():
        if k == 'Wq':
            out['Wq_bytes'] = e4m3fn_bytes(x0 / s.astype(np.float64))
            out['Wq_scale'] = s
        else:
            out[k] = v
    return out


def reference(hidden_states, Wq_bytes, Wq_scale, Wk, Wv):
    return core(hidden_states, e4m3fn_values(Wq_bytes) * Wq_scale.astype(np.float64), Wk, Wv)

@@ -1,0 +1,220 @@
+import math
+from contextlib import ExitStack
+
+import concourse.mybir as mybir
+from concourse.masks import make_identity
+
+F32 = mybir.dt.float32
+BF16 = mybir.dt.bfloat16
+U8 = mybir.dt.uint8
+U32 = mybir.dt.uint32
+I32 = mybir.dt.int32
+FP8 = mybir.dt.float8_e4m3fn
+FP8X4 = mybir.dt.float8_e4m3fn_x4
+ALU = mybir.AluOpType
+ACT = mybir.ActivationFunctionType
+
+P = 128
+TOKENS = 1024
+K = 1536
+PASSES = 3
+HD = 128
+ROT = 96
+HALF = 48
+BASE = 10000.0
+NB = 512
+
+FLOPS = 2 * TOKENS * K * 2560
+
+INTERLEAVE = {
+    "q0": "vvv", "q1": "aaa", "q2": "aaa", "k": "aaa", "v": "aaa",
+}
+GROUPS = ("q0", "q1", "q2", "v", "k")
+
+
+def tile_phi4miniattention_pa_kernel(tc, hidden_states, Wq_bytes, Wq_scale, Wk, Wv, out_0, out_1, out_2):
+    nc = tc.nc
+    with ExitStack() as ctx:
+        keep = ctx.enter_context(tc.tile_pool(name="keep", bufs=1))
+        stage = ctx.enter_context(tc.tile_pool(name="stage", bufs=3))
+        work = ctx.enter_context(tc.tile_pool(name="work", bufs=4))
+        psum = ctx.enter_context(tc.psum_pool(name="psum", bufs=8))
+
+        hs = hidden_states.rearrange("b s k -> (b s) k")
+        wq_v = Wq_bytes.rearrange("(g p t) h d -> g p t (h d)", p=P, t=4)
+        wk_v = Wk.rearrange("(g p t) h d -> g p t (h d)", p=P, t=4)
+        wv_v = Wv.rearrange("(g p t) h d -> g p t (h d)", p=P, t=4)
+
+        sc = keep.tile([P, PASSES, 4], F32, name="sc")
+        nc.sync.dma_start(out=sc[:], in_=Wq_scale.rearrange("(g p t) a b -> p g (t a b)", p=P, t=4))
+
+        x_sb = []
+        for m in range(8):
+            x_t = keep.tile([P, K], BF16, name="x%d" % m)
+            x_sb.append(x_t)
+        wq_bytes_sb = {}
+        for cq in range(3):
+            for g in range(PASSES):
+                b_t = keep.tile([P, 4, NB], U8, name="wqbytes%d_%d" % (cq, g))
+                wq_bytes_sb[(cq, g)] = b_t
+        raw = {}
+        for grp in ("k", "v"):
+            for g in range(PASSES):
+                r_t = keep.tile([P, 4, NB], BF16, name="raw%s%d" % (grp, g))
+                raw[(grp, g)] = r_t
+
+        def load_x(m):
+            nc.sync.dma_start(out=x_sb[m][:], in_=hs[P * m:P * (m + 1), :])
+
+        def load_wq(cq, g):
+            nc.sync.dma_start(out=wq_bytes_sb[(cq, g)][:], in_=wq_v[g][:, :, NB * cq:NB * (cq + 1)])
+
+        load_wq(0, 0)
+        load_x(0)
+        load_x(1)
+        load_wq(0, 1)
+        load_x(2)
+        load_x(3)
+        load_wq(0, 2)
+        for m in range(4, 8):
+            load_x(m)
+        for cq in (1, 2):
+            for g in range(PASSES):
+                load_wq(cq, g)
+        for g in range(PASSES):
+            nc.sync.dma_start(out=raw[("k", g)][:], in_=wk_v[g])
+        for g in range(PASSES):
+            nc.sync.dma_start(out=raw[("v", g)][:], in_=wv_v[g])
+
+        zero1 = keep.tile([P, 1], F32, name="zero1")
+        nc.gpsimd.memset(zero1[:], 0.0)
+        warm = keep.tile([P, 1], F32, name="warm")
+        nc.scalar.activation(out=warm[:], in_=zero1[:], func=ACT.Sin)
+
+        pos = keep.tile([P, 4], F32, name="pos")
+        nc.gpsimd.iota(pos[:], pattern=[[P, 4]], base=0, channel_multiplier=1, allow_small_or_imprecise_dtypes=True)
+        ident = keep.tile([P, P], F32, name="ident")
+        make_identity(nc, ident[:])
+
+        with tc.high_priority():
+            theta = keep.tile([P, 4, HALF], F32, name="theta")
+            nc.vector.tensor_copy(out=theta[:, :, 0:1], in_=pos[:].unsqueeze(2))
+            for s in (1, 2, 4, 8, 16):
+                nc.vector.tensor_scalar(out=theta[:, :, s:2 * s], in0=theta[:, :, 0:s], scalar1=BASE ** (-s / 48.0), scalar2=None, op0=ALU.mult)
+            nc.vector.tensor_scalar(out=theta[:, :, 32:48], in0=theta[:, :, 0:16], scalar1=BASE ** (-32 / 48.0), scalar2=None, op0=ALU.mult)
+            turns_i = keep.tile([P, 4, HALF], I32, name="turns_i")
+            nc.vector.tensor_scalar(out=turns_i[:], in0=theta[:], scalar1=1.0 / (2.0 * math.pi), scalar2=None, op0=ALU.mult)
+            turns = keep.tile([P, 4, HALF], F32, name="turns")
+            nc.vector.tensor_copy(out=turns[:], in_=turns_i[:])
+            c_hi = 6.28125
+            c_lo = 2.0 * math.pi - c_hi
+            red = keep.tile([P, 4, HALF], F32, name="red")
+            nc.vector.scalar_tensor_tensor(out=red[:], in0=turns[:], scalar=-c_hi, in1=theta[:], op0=ALU.mult, op1=ALU.add)
+            args = keep.tile([P, 2, 4, HALF], F32, name="args")
+            nc.vector.scalar_tensor_tensor(out=args[:, 0], in0=turns[:], scalar=-c_lo, in1=red[:], op0=ALU.mult, op1=ALU.add)
+            nc.vector.tensor_scalar(out=args[:, 1], in0=args[:, 0], scalar1=-0.5 * math.pi, scalar2=None, op0=ALU.add)
+            halfsin = keep.tile([P, 2, 4, HALF], F32, name="halfsin")
+            nc.scalar.activation(out=halfsin[:], in_=args[:], func=ACT.Sin, scale=0.5)
+            sq = keep.tile([P, 2, 4, HALF], F32, name="sq")
+            nc.vector.tensor_tensor(out=sq[:], in0=halfsin[:], in1=halfsin[:], op=ALU.mult)
+            rot = keep.tile([P, 4, 2, 2, HALF], F32, name="rot")
+            nc.vector.tensor_scalar(out=rot[:, :, 0, 0, :], in0=sq[:, 0], scalar1=-2.0, scalar2=1.0, op0=ALU.mult, op1=ALU.add)
+            nc.vector.tensor_scalar(out=rot[:, :, 1, 1, :], in0=sq[:, 0], scalar1=-2.0, scalar2=1.0, op0=ALU.mult, op1=ALU.add)
+            nc.vector.tensor_scalar(out=rot[:, :, 1, 0, :], in0=sq[:, 1], scalar1=-2.0, scalar2=1.0, op0=ALU.mult, op1=ALU.add)
+            nc.vector.tensor_scalar(out=rot[:, :, 0, 1, :], in0=sq[:, 1], scalar1=2.0, scalar2=-1.0, op0=ALU.mult, op1=ALU.add)
+
+        xg = []
+        xc = []
+        xs = []
+        for g in range(PASSES):
+            xg_t = keep.tile([P, 4 * TOKENS], BF16, name="xg%d" % g, align_bytes=64)
+            xc_t = keep.tile([P, TOKENS], U32, name="xc%d" % g, align_bytes=64)
+            xs_t = keep.tile([P, TOKENS], U8, name="xs%d" % g, align_bytes=64)
+            xg.append(xg_t)
+            xc.append(xc_t)
+            xs.append(xs_t)
+        for i in range(4):
+            for g in range(PASSES):
+                xt = psum.tile([P, 2, 2, P], F32, name="xt", tag="bank")
+                for c in range(2):
+                    words = x_sb[2 * i + c][:].bitcast(F32)
+                    for u in range(2):
+                        nc.tensor.transpose(xt[:, c, u, :], words[:, 256 * g + u:256 * (g + 1):2], ident[:])
+                dst = xg[g][:].bitcast(F32)[:, 512 * i:512 * (i + 1)].rearrange("p (c r u) -> p c r u", c=2, u=2)
+                nc.scalar.copy(out=dst, in_=xt[:].rearrange("p c u r -> p c r u"))
+                nc.vector.quantize_mx(
+                    out=xc[g][:, 256 * i:256 * (i + 1)].bitcast(FP8X4),
+                    scales=xs[g][:, 256 * i:256 * (i + 1)],
+                    in_=xg[g][:, 1024 * i:1024 * (i + 1)],
+                )
+
+        outs = {
+            "q0": out_0.rearrange("b s h d -> (b s) (h d)")[:, 0:NB],
+            "q1": out_0.rearrange("b s h d -> (b s) (h d)")[:, NB:2 * NB],
+            "q2": out_0.rearrange("b s h d -> (b s) (h d)")[:, 2 * NB:3 * NB],
+            "k": out_1.rearrange("b s h d -> (b s) (h d)"),
+            "v": out_2.rearrange("b s h d -> (b s) (h d)"),
+        }
+        for grp in GROUPS:
+            wc = keep.tile([P, PASSES, NB], U32, name="wc_" + grp, align_bytes=64)
+            ws = keep.tile([P, PASSES, NB], U8, name="ws_" + grp, align_bytes=64)
+            for g in range(PASSES):
+                if grp in ("k", "v"):
+                    src = raw[(grp, g)]
+                else:
+                    cq = ("q0", "q1", "q2").index(grp)
+                    src = stage.tile([P, 4, NB], BF16, name="wide", tag="wide")
+                    for t in range(4):
+                        nc.scalar.activation(
+                            out=src[:, t, :],
+                            in_=wq_bytes_sb[(cq, g)][:, t, :].bitcast(FP8),
+                            func=ACT.Copy,
+                            scale=sc[:, g, t:t + 1],
+                        )
+                wg = stage.tile([P, NB, 4], BF16, name="wg", tag="wg", align_bytes=64)
+                if INTERLEAVE[grp][g] == "v":
+                    nc.vector.tensor_copy(out=wg[:], in_=src[:].rearrange("p t n -> p n t"))
+                elif INTERLEAVE[grp][g] == "a":
+                    nc.any.tensor_copy(out=wg[:], in_=src[:].rearrange("p t n -> p n t"))
+                else:
+                    nc.scalar.copy(out=wg[:], in_=src[:].rearrange("p t n -> p n t"))
+                nc.vector.quantize_mx(
+                    out=wc[:, g, :].bitcast(FP8X4),
+                    scales=ws[:, g, :],
+                    in_=wg[:].rearrange("p n t -> p (n t)"),
+                )
+            for m in range(8):
+                acc = psum.tile([P, NB], F32, name="acc", tag="bank")
+                for g in range(PASSES):
+                    nc.tensor.matmul_mx(
+                        out=acc[:],
+                        lhsT=xc[g][:, P * m:P * (m + 1)].bitcast(FP8X4),
+                        lhsT_scale=xs[g][:, P * m:P * (m + 1)],
+                        rhs=wc[:, g, :].bitcast(FP8X4),
+                        rhs_scale=ws[:, g, :],
+                        start=(g == 0),
+                        stop=(g == PASSES - 1),
+                    )
+                o = work.tile([P, NB], F32, name="o", tag="o")
+                if grp == "v":
+                    nc.any.tensor_copy(out=o[:], in_=acc[:])
+                else:
+                    a = m % 4
+                    y = acc[:].rearrange("p (h d) -> p h d", h=4)
+                    oh = o[:].rearrange("p (h d) -> p h d", h=4)
+                    z = work.tile([P, 4, 2, ROT], F32, name="z", tag="z")
+                    nc.vector.tensor_tensor(
+                        out=z[:],
+                        in0=y[:, :, 0:ROT].unsqueeze(2).to_broadcast([P, 4, 2, ROT]),
+                        in1=rot[:, a].rearrange("p r f j -> p r (f j)").unsqueeze(1).to_broadcast([P, 4, 2, ROT]),
+                        op=ALU.mult,
+                    )
+                    nc.scalar.copy(out=oh[:, :, ROT:HD], in_=y[:, :, ROT:HD])
+                    zv = z[:].rearrange("p h r (f j) -> p h r f j", f=2)
+                    nc.vector.tensor_tensor(
+                        out=oh[:, :, 0:ROT].rearrange("p h (r j) -> p h r j", r=2),
+                        in0=zv[:, :, :, 0, :],
+                        in1=zv[:, :, :, 1, :],
+                        op=ALU.add,
+                    )
+                nc.sync.dma_start(out=outs[grp][P * m:P * (m + 1), :], in_=o[:])

@@ -37,7 +37,7 @@ def tile_phi4miniattention_pa_kernel(tc, hidden_states, Wq_bytes, Wq_scale, Wk, 
     with ExitStack() as ctx:
         keep = ctx.enter_context(tc.tile_pool(name="keep", bufs=1))
         stage = ctx.enter_context(tc.tile_pool(name="stage", bufs=3))
-        work = ctx.enter_context(tc.tile_pool(name="work", bufs=4))
+        work = ctx.enter_context(tc.tile_pool(name="work", bufs=6))
         psum = ctx.enter_context(tc.psum_pool(name="psum", bufs=8))
 
         hs = hidden_states.rearrange("b s k -> (b s) k")
@@ -211,7 +211,7 @@ def tile_phi4miniattention_pa_kernel(tc, hidden_states, Wq_bytes, Wq_scale, Wk, 
                     )
                     nc.scalar.copy(out=oh[:, :, ROT:HD], in_=y[:, :, ROT:HD])
                     zv = z[:].rearrange("p h r (f j) -> p h r f j", f=2)
-                    nc.vector.tensor_tensor(
+                    nc.gpsimd.tensor_tensor(
                         out=oh[:, :, 0:ROT].rearrange("p h (r j) -> p h r j", r=2),
                         in0=zv[:, :, :, 0, :],
                         in1=zv[:, :, :, 1, :],

@@ -27,7 +27,7 @@ NB = 512
 FLOPS = 2 * TOKENS * K * 2560
 
 INTERLEAVE = {
-    "q0": "vvv", "q1": "aaa", "q2": "aaa", "k": "aaa", "v": "aaa",
+    "q0": "vvv", "q1": "vvv", "q2": "vvs", "k": "sss", "v": "sss",
 }
 GROUPS = ("q0", "q1", "q2", "v", "k")
 
@@ -95,33 +95,40 @@ def tile_phi4miniattention_pa_kernel(tc, hidden_states, Wq_bytes, Wq_scale, Wk, 
         nc.gpsimd.iota(pos[:], pattern=[[P, 4]], base=0, channel_multiplier=1, allow_small_or_imprecise_dtypes=True)
         ident = keep.tile([P, P], F32, name="ident")
         make_identity(nc, ident[:])
+        ident_bf = keep.tile([P, P], BF16, name="ident_bf")
+        make_identity(nc, ident_bf[:])
 
-        with tc.high_priority():
-            theta = keep.tile([P, 4, HALF], F32, name="theta")
-            nc.vector.tensor_copy(out=theta[:, :, 0:1], in_=pos[:].unsqueeze(2))
-            for s in (1, 2, 4, 8, 16):
-                nc.vector.tensor_scalar(out=theta[:, :, s:2 * s], in0=theta[:, :, 0:s], scalar1=BASE ** (-s / 48.0), scalar2=None, op0=ALU.mult)
-            nc.vector.tensor_scalar(out=theta[:, :, 32:48], in0=theta[:, :, 0:16], scalar1=BASE ** (-32 / 48.0), scalar2=None, op0=ALU.mult)
-            turns_i = keep.tile([P, 4, HALF], I32, name="turns_i")
-            nc.vector.tensor_scalar(out=turns_i[:], in0=theta[:], scalar1=1.0 / (2.0 * math.pi), scalar2=None, op0=ALU.mult)
-            turns = keep.tile([P, 4, HALF], F32, name="turns")
-            nc.vector.tensor_copy(out=turns[:], in_=turns_i[:])
-            c_hi = 6.28125
-            c_lo = 2.0 * math.pi - c_hi
-            red = keep.tile([P, 4, HALF], F32, name="red")
-            nc.vector.scalar_tensor_tensor(out=red[:], in0=turns[:], scalar=-c_hi, in1=theta[:], op0=ALU.mult, op1=ALU.add)
-            args = keep.tile([P, 2, 4, HALF], F32, name="args")
-            nc.vector.scalar_tensor_tensor(out=args[:, 0], in0=turns[:], scalar=-c_lo, in1=red[:], op0=ALU.mult, op1=ALU.add)
-            nc.vector.tensor_scalar(out=args[:, 1], in0=args[:, 0], scalar1=-0.5 * math.pi, scalar2=None, op0=ALU.add)
-            halfsin = keep.tile([P, 2, 4, HALF], F32, name="halfsin")
-            nc.scalar.activation(out=halfsin[:], in_=args[:], func=ACT.Sin, scale=0.5)
-            sq = keep.tile([P, 2, 4, HALF], F32, name="sq")
-            nc.vector.tensor_tensor(out=sq[:], in0=halfsin[:], in1=halfsin[:], op=ALU.mult)
-            rot = keep.tile([P, 4, 2, 2, HALF], F32, name="rot")
-            nc.vector.tensor_scalar(out=rot[:, :, 0, 0, :], in0=sq[:, 0], scalar1=-2.0, scalar2=1.0, op0=ALU.mult, op1=ALU.add)
-            nc.vector.tensor_scalar(out=rot[:, :, 1, 1, :], in0=sq[:, 0], scalar1=-2.0, scalar2=1.0, op0=ALU.mult, op1=ALU.add)
-            nc.vector.tensor_scalar(out=rot[:, :, 1, 0, :], in0=sq[:, 1], scalar1=-2.0, scalar2=1.0, op0=ALU.mult, op1=ALU.add)
-            nc.vector.tensor_scalar(out=rot[:, :, 0, 1, :], in0=sq[:, 1], scalar1=2.0, scalar2=-1.0, op0=ALU.mult, op1=ALU.add)
+        def g_scale(out, in0, factor, shift=0.0):
+            nc.gpsimd.tensor_scalar(out=out, in0=in0, scalar1=factor, scalar2=shift, op0=ALU.mult, op1=ALU.add)
+
+        theta = keep.tile([P, 4, HALF], F32, name="theta")
+        g_scale(theta[:, :, 0:1], pos[:].unsqueeze(2), 1.0)
+        for s in (1, 2, 4, 8, 16):
+            g_scale(theta[:, :, s:2 * s], theta[:, :, 0:s], BASE ** (-s / 48.0))
+        g_scale(theta[:, :, 32:48], theta[:, :, 0:16], BASE ** (-32 / 48.0))
+        turns_i = keep.tile([P, 4, HALF], I32, name="turns_i")
+        g_scale(turns_i[:], theta[:], 1.0 / (2.0 * math.pi))
+        turns = keep.tile([P, 4, HALF], F32, name="turns")
+        nc.vector.tensor_copy(out=turns[:], in_=turns_i[:])
+        c_hi = 6.28125
+        c_lo = 2.0 * math.pi - c_hi
+        back = keep.tile([P, 2, 4, HALF], F32, name="back")
+        g_scale(back[:, 0], turns[:], -c_hi)
+        g_scale(back[:, 1], turns[:], -c_lo)
+        red = keep.tile([P, 4, HALF], F32, name="red")
+        nc.gpsimd.tensor_tensor(out=red[:], in0=theta[:], in1=back[:, 0], op=ALU.add)
+        args = keep.tile([P, 2, 4, HALF], F32, name="args")
+        nc.gpsimd.tensor_tensor(out=args[:, 0], in0=red[:], in1=back[:, 1], op=ALU.add)
+        g_scale(args[:, 1], args[:, 0], 1.0, -0.5 * math.pi)
+        halfsin = keep.tile([P, 2, 4, HALF], F32, name="halfsin")
+        nc.scalar.activation(out=halfsin[:], in_=args[:], func=ACT.Sin, scale=0.5)
+        sq = keep.tile([P, 2, 4, HALF], F32, name="sq")
+        nc.gpsimd.tensor_tensor(out=sq[:], in0=halfsin[:], in1=halfsin[:], op=ALU.mult)
+        rot = keep.tile([P, 4, 2, 2, HALF], F32, name="rot")
+        g_scale(rot[:, :, 0, 0, :], sq[:, 0], -2.0, 1.0)
+        g_scale(rot[:, :, 1, 1, :], sq[:, 0], -2.0, 1.0)
+        g_scale(rot[:, :, 1, 0, :], sq[:, 1], -2.0, 1.0)
+        g_scale(rot[:, :, 0, 1, :], sq[:, 1], 2.0, -1.0)
 
         xg = []
         xc = []
@@ -172,12 +179,26 @@ def tile_phi4miniattention_pa_kernel(tc, hidden_states, Wq_bytes, Wq_scale, Wk, 
                             scale=sc[:, g, t:t + 1],
                         )
                 wg = stage.tile([P, NB, 4], BF16, name="wg", tag="wg", align_bytes=64)
-                if INTERLEAVE[grp][g] == "v":
+                if INTERLEAVE[grp][g] == "p":
+                    wg_flat = wg[:].rearrange("p n t -> p (n t)")
+                    for h in range(2):
+                        pb = psum.tile([P, 1024], BF16, name="pb", tag="bank")
+                        for q in range(2):
+                            n0 = 256 * h + 128 * q
+                            nc.tensor.matmul(
+                                out=pb[:, 512 * q:512 * (q + 1)].rearrange("p (n t) -> p n t", t=4),
+                                lhsT=ident_bf[:],
+                                rhs=src[:, :, n0:n0 + 128].rearrange("p t n -> p n t"),
+                                start=True,
+                                stop=True,
+                            )
+                        nc.scalar.copy(out=wg_flat[:, 1024 * h:1024 * (h + 1)], in_=pb[:])
+                elif INTERLEAVE[grp][g] == "v":
                     nc.vector.tensor_copy(out=wg[:], in_=src[:].rearrange("p t n -> p n t"))
                 elif INTERLEAVE[grp][g] == "a":
-                    nc.any.tensor_copy(out=wg[:], in_=src[:].rearrange("p t n -> p n t"))
+                    nc.any.tensor_copy(out=wg[:].rearrange("p (c i) t -> p c t i", i=4), in_=src[:].rearrange("p t (c i) -> p c t i", i=4))
                 else:
-                    nc.scalar.copy(out=wg[:], in_=src[:].rearrange("p t n -> p n t"))
+                    nc.scalar.copy(out=wg[:].rearrange("p (c i) t -> p c t i", i=4), in_=src[:].rearrange("p t (c i) -> p c t i", i=4))
                 nc.vector.quantize_mx(
                     out=wc[:, g, :].bitcast(FP8X4),
                     scales=ws[:, g, :],
@@ -197,7 +218,7 @@ def tile_phi4miniattention_pa_kernel(tc, hidden_states, Wq_bytes, Wq_scale, Wk, 
                     )
                 o = work.tile([P, NB], F32, name="o", tag="o")
                 if grp == "v":
-                    nc.any.tensor_copy(out=o[:], in_=acc[:])
+                    nc.scalar.copy(out=o[:], in_=acc[:])
                 else:
                     a = m % 4
                     y = acc[:].rearrange("p (h d) -> p h d", h=4)
@@ -211,7 +232,8 @@ def tile_phi4miniattention_pa_kernel(tc, hidden_states, Wq_bytes, Wq_scale, Wk, 
                     )
                     nc.scalar.copy(out=oh[:, :, ROT:HD], in_=y[:, :, ROT:HD])
                     zv = z[:].rearrange("p h r (f j) -> p h r f j", f=2)
-                    nc.gpsimd.tensor_tensor(
+                    add_engine = nc.gpsimd if (grp == GROUPS[-1] and m < 6) else nc.vector
+                    add_engine.tensor_tensor(
                         out=oh[:, :, 0:ROT].rearrange("p h (r j) -> p h r j", r=2),
                         in0=zv[:, :, :, 0, :],
                         in1=zv[:, :, :, 1, :],

@@ -27,7 +27,7 @@ NB = 512
 FLOPS = 2 * TOKENS * K * 2560
 
 INTERLEAVE = {
-    "q0": "vvv", "q1": "vvv", "q2": "vvs", "k": "sss", "v": "sss",
+    "q0": "vvv", "q1": "aaa", "q2": "aaa", "k": "aaa", "v": "aaa",
 }
 GROUPS = ("q0", "q1", "q2", "v", "k")
 
@@ -37,7 +37,7 @@ def tile_phi4miniattention_pa_kernel(tc, hidden_states, Wq_bytes, Wq_scale, Wk, 
     with ExitStack() as ctx:
         keep = ctx.enter_context(tc.tile_pool(name="keep", bufs=1))
         stage = ctx.enter_context(tc.tile_pool(name="stage", bufs=3))
-        work = ctx.enter_context(tc.tile_pool(name="work", bufs=6))
+        work = ctx.enter_context(tc.tile_pool(name="work", bufs=4))
         psum = ctx.enter_context(tc.psum_pool(name="psum", bufs=8))
 
         hs = hidden_states.rearrange("b s k -> (b s) k")
@@ -95,40 +95,33 @@ def tile_phi4miniattention_pa_kernel(tc, hidden_states, Wq_bytes, Wq_scale, Wk, 
         nc.gpsimd.iota(pos[:], pattern=[[P, 4]], base=0, channel_multiplier=1, allow_small_or_imprecise_dtypes=True)
         ident = keep.tile([P, P], F32, name="ident")
         make_identity(nc, ident[:])
-        ident_bf = keep.tile([P, P], BF16, name="ident_bf")
-        make_identity(nc, ident_bf[:])
 
-        def g_scale(out, in0, factor, shift=0.0):
-            nc.gpsimd.tensor_scalar(out=out, in0=in0, scalar1=factor, scalar2=shift, op0=ALU.mult, op1=ALU.add)
-
-        theta = keep.tile([P, 4, HALF], F32, name="theta")
-        g_scale(theta[:, :, 0:1], pos[:].unsqueeze(2), 1.0)
-        for s in (1, 2, 4, 8, 16):
-            g_scale(theta[:, :, s:2 * s], theta[:, :, 0:s], BASE ** (-s / 48.0))
-        g_scale(theta[:, :, 32:48], theta[:, :, 0:16], BASE ** (-32 / 48.0))
-        turns_i = keep.tile([P, 4, HALF], I32, name="turns_i")
-        g_scale(turns_i[:], theta[:], 1.0 / (2.0 * math.pi))
-        turns = keep.tile([P, 4, HALF], F32, name="turns")
-        nc.vector.tensor_copy(out=turns[:], in_=turns_i[:])
-        c_hi = 6.28125
-        c_lo = 2.0 * math.pi - c_hi
-        back = keep.tile([P, 2, 4, HALF], F32, name="back")
-        g_scale(back[:, 0], turns[:], -c_hi)
-        g_scale(back[:, 1], turns[:], -c_lo)
-        red = keep.tile([P, 4, HALF], F32, name="red")
-        nc.gpsimd.tensor_tensor(out=red[:], in0=theta[:], in1=back[:, 0], op=ALU.add)
-        args = keep.tile([P, 2, 4, HALF], F32, name="args")
-        nc.gpsimd.tensor_tensor(out=args[:, 0], in0=red[:], in1=back[:, 1], op=ALU.add)
-        g_scale(args[:, 1], args[:, 0], 1.0, -0.5 * math.pi)
-        halfsin = keep.tile([P, 2, 4, HALF], F32, name="halfsin")
-        nc.scalar.activation(out=halfsin[:], in_=args[:], func=ACT.Sin, scale=0.5)
-        sq = keep.tile([P, 2, 4, HALF], F32, name="sq")
-        nc.gpsimd.tensor_tensor(out=sq[:], in0=halfsin[:], in1=halfsin[:], op=ALU.mult)
-        rot = keep.tile([P, 4, 2, 2, HALF], F32, name="rot")
-        g_scale(rot[:, :, 0, 0, :], sq[:, 0], -2.0, 1.0)
-        g_scale(rot[:, :, 1, 1, :], sq[:, 0], -2.0, 1.0)
-        g_scale(rot[:, :, 1, 0, :], sq[:, 1], -2.0, 1.0)
-        g_scale(rot[:, :, 0, 1, :], sq[:, 1], 2.0, -1.0)
+        with tc.high_priority():
+            theta = keep.tile([P, 4, HALF], F32, name="theta")
+            nc.vector.tensor_copy(out=theta[:, :, 0:1], in_=pos[:].unsqueeze(2))
+            for s in (1, 2, 4, 8, 16):
+                nc.vector.tensor_scalar(out=theta[:, :, s:2 * s], in0=theta[:, :, 0:s], scalar1=BASE ** (-s / 48.0), scalar2=None, op0=ALU.mult)
+            nc.vector.tensor_scalar(out=theta[:, :, 32:48], in0=theta[:, :, 0:16], scalar1=BASE ** (-32 / 48.0), scalar2=None, op0=ALU.mult)
+            turns_i = keep.tile([P, 4, HALF], I32, name="turns_i")
+            nc.vector.tensor_scalar(out=turns_i[:], in0=theta[:], scalar1=1.0 / (2.0 * math.pi), scalar2=None, op0=ALU.mult)
+            turns = keep.tile([P, 4, HALF], F32, name="turns")
+            nc.vector.tensor_copy(out=turns[:], in_=turns_i[:])
+            c_hi = 6.28125
+            c_lo = 2.0 * math.pi - c_hi
+            red = keep.tile([P, 4, HALF], F32, name="red")
+            nc.vector.scalar_tensor_tensor(out=red[:], in0=turns[:], scalar=-c_hi, in1=theta[:], op0=ALU.mult, op1=ALU.add)
+            args = keep.tile([P, 2, 4, HALF], F32, name="args")
+            nc.vector.scalar_tensor_tensor(out=args[:, 0], in0=turns[:], scalar=-c_lo, in1=red[:], op0=ALU.mult, op1=ALU.add)
+            nc.vector.tensor_scalar(out=args[:, 1], in0=args[:, 0], scalar1=-0.5 * math.pi, scalar2=None, op0=ALU.add)
+            halfsin = keep.tile([P, 2, 4, HALF], F32, name="halfsin")
+            nc.scalar.activation(out=halfsin[:], in_=args[:], func=ACT.Sin, scale=0.5)
+            sq = keep.tile([P, 2, 4, HALF], F32, name="sq")
+            nc.vector.tensor_tensor(out=sq[:], in0=halfsin[:], in1=halfsin[:], op=ALU.mult)
+            rot = keep.tile([P, 4, 2, 2, HALF], F32, name="rot")
+            nc.vector.tensor_scalar(out=rot[:, :, 0, 0, :], in0=sq[:, 0], scalar1=-2.0, scalar2=1.0, op0=ALU.mult, op1=ALU.add)
+            nc.vector.tensor_scalar(out=rot[:, :, 1, 1, :], in0=sq[:, 0], scalar1=-2.0, scalar2=1.0, op0=ALU.mult, op1=ALU.add)
+            nc.vector.tensor_scalar(out=rot[:, :, 1, 0, :], in0=sq[:, 1], scalar1=-2.0, scalar2=1.0, op0=ALU.mult, op1=ALU.add)
+            nc.vector.tensor_scalar(out=rot[:, :, 0, 1, :], in0=sq[:, 1], scalar1=2.0, scalar2=-1.0, op0=ALU.mult, op1=ALU.add)
 
         xg = []
         xc = []
@@ -162,6 +155,15 @@ def tile_phi4miniattention_pa_kernel(tc, hidden_states, Wq_bytes, Wq_scale, Wk, 
             "k": out_1.rearrange("b s h d -> (b s) (h d)"),
             "v": out_2.rearrange("b s h d -> (b s) (h d)"),
         }
+        waiting = {}
+
+        def finish_bank():
+            if "bank" in waiting:
+                p_out, p_in0, p_in1, p_dram, p_tile = waiting["bank"]
+                nc.vector.tensor_tensor(out=p_out, in0=p_in0, in1=p_in1, op=ALU.add)
+                nc.sync.dma_start(out=p_dram, in_=p_tile)
+                waiting.clear()
+
         for grp in GROUPS:
             wc = keep.tile([P, PASSES, NB], U32, name="wc_" + grp, align_bytes=64)
             ws = keep.tile([P, PASSES, NB], U8, name="ws_" + grp, align_bytes=64)
@@ -179,26 +181,12 @@ def tile_phi4miniattention_pa_kernel(tc, hidden_states, Wq_bytes, Wq_scale, Wk, 
                             scale=sc[:, g, t:t + 1],
                         )
                 wg = stage.tile([P, NB, 4], BF16, name="wg", tag="wg", align_bytes=64)
-                if INTERLEAVE[grp][g] == "p":
-                    wg_flat = wg[:].rearrange("p n t -> p (n t)")
-                    for h in range(2):
-                        pb = psum.tile([P, 1024], BF16, name="pb", tag="bank")
-                        for q in range(2):
-                            n0 = 256 * h + 128 * q
-                            nc.tensor.matmul(
-                                out=pb[:, 512 * q:512 * (q + 1)].rearrange("p (n t) -> p n t", t=4),
-                                lhsT=ident_bf[:],
-                                rhs=src[:, :, n0:n0 + 128].rearrange("p t n -> p n t"),
-                                start=True,
-                                stop=True,
-                            )
-                        nc.scalar.copy(out=wg_flat[:, 1024 * h:1024 * (h + 1)], in_=pb[:])
-                elif INTERLEAVE[grp][g] == "v":
+                if INTERLEAVE[grp][g] == "v":
                     nc.vector.tensor_copy(out=wg[:], in_=src[:].rearrange("p t n -> p n t"))
                 elif INTERLEAVE[grp][g] == "a":
-                    nc.any.tensor_copy(out=wg[:].rearrange("p (c i) t -> p c t i", i=4), in_=src[:].rearrange("p t (c i) -> p c t i", i=4))
+                    nc.any.tensor_copy(out=wg[:], in_=src[:].rearrange("p t n -> p n t"))
                 else:
-                    nc.scalar.copy(out=wg[:].rearrange("p (c i) t -> p c t i", i=4), in_=src[:].rearrange("p t (c i) -> p c t i", i=4))
+                    nc.scalar.copy(out=wg[:], in_=src[:].rearrange("p t n -> p n t"))
                 nc.vector.quantize_mx(
                     out=wc[:, g, :].bitcast(FP8X4),
                     scales=ws[:, g, :],
@@ -218,7 +206,7 @@ def tile_phi4miniattention_pa_kernel(tc, hidden_states, Wq_bytes, Wq_scale, Wk, 
                     )
                 o = work.tile([P, NB], F32, name="o", tag="o")
                 if grp == "v":
-                    nc.scalar.copy(out=o[:], in_=acc[:])
+                    nc.any.tensor_copy(out=o[:], in_=acc[:])
                 else:
                     a = m % 4
                     y = acc[:].rearrange("p (h d) -> p h d", h=4)
@@ -232,11 +220,14 @@ def tile_phi4miniattention_pa_kernel(tc, hidden_states, Wq_bytes, Wq_scale, Wk, 
                     )
                     nc.scalar.copy(out=oh[:, :, ROT:HD], in_=y[:, :, ROT:HD])
                     zv = z[:].rearrange("p h r (f j) -> p h r f j", f=2)
-                    add_engine = nc.gpsimd if (grp == GROUPS[-1] and m < 6) else nc.vector
-                    add_engine.tensor_tensor(
-                        out=oh[:, :, 0:ROT].rearrange("p h (r j) -> p h r j", r=2),
-                        in0=zv[:, :, :, 0, :],
-                        in1=zv[:, :, :, 1, :],
-                        op=ALU.add,
+                    finish_bank()
+                    waiting["bank"] = (
+                        oh[:, :, 0:ROT].rearrange("p h (r j) -> p h r j", r=2),
+                        zv[:, :, :, 0, :],
+                        zv[:, :, :, 1, :],
+                        outs[grp][P * m:P * (m + 1), :],
+                        o[:],
                     )
-                nc.sync.dma_start(out=outs[grp][P * m:P * (m + 1), :], in_=o[:])
+                if grp == "v":
+                    nc.sync.dma_start(out=outs[grp][P * m:P * (m + 1), :], in_=o[:])
+            finish_bank()

@@ -26,128 +26,184 @@ NB = 512
 
 FLOPS = 2 * TOKENS * K * 2560
 
-INTERLEAVE = {
-    "q0": "vvv", "q1": "aaa", "q2": "aaa", "k": "aaa", "v": "aaa",
-}
-GROUPS = ("q0", "q1", "q2", "v", "k")
+ROPE_GROUPS = ("k", "q0", "q1", "q2")
+INTERLEAVE = {"k": "VVV", "q0": "VVV", "q1": "VSS", "q2": "SSS", "v": "VVV"}
+LATE = "q2"
+WIDE_BUFS = 4
+WG_BUFS = 3
+XG_BUFS = 6
+Z_BUFS = 6
+O_BUFS = 8
+
+
+def engine_lists():
+    lists = {"D": [], "G": [], "P": [], "S": [], "V": []}
+    needs = {}
+
+    def step(engine, name, before):
+        lists[engine].append(name)
+        needs[name] = before
+
+    def source(grp, g):
+        if grp in ("k", "v"):
+            return ("L", grp, g)
+        return ("W", grp, g)
+
+    def widen(grp, g):
+        step("S", ("W", grp, g), [("L", grp, g), ("L", "sc", 0)])
+
+    def interleave(grp, g):
+        step(INTERLEAVE[grp][g], ("I", grp, g), [source(grp, g)])
+
+    step("D", ("L", "sc", 0), [])
+    for g in range(PASSES):
+        step("D", ("L", "k", g), [])
+        step("D", ("L", "q0", g), [])
+    for g in range(PASSES):
+        step("D", ("L", "x", 2 * g), [])
+        step("D", ("L", "x", 2 * g + 1), [])
+        step("D", ("L", "q1", g), [])
+        step("D", ("L", "v", g), [])
+    step("D", ("L", "x", 6), [])
+    step("D", ("L", "x", 7), [])
+    for g in range(PASSES):
+        step("D", ("L", LATE, g), [])
+
+    step("G", ("const", "", 0), [])
+    step("S", ("warm", "", 0), [("const", "", 0)])
+    step("V", ("tab1", "", 0), [("const", "", 0)])
+    step("S", ("sin", "", 0), [("tab1", "", 0)])
+
+    for i in range(4):
+        step("P", ("T", "x", i), [("L", "x", 2 * i), ("L", "x", 2 * i + 1), ("const", "", 0)])
+    for g in range(PASSES):
+        widen("q0", g)
+    for i in range(PASSES):
+        step("S", ("C", "x", i), [("T", "x", i)])
+        widen("q1", i)
+        if INTERLEAVE["q1"][i] == "S":
+            interleave("q1", i)
+    step("S", ("C", "x", 3), [("T", "x", 3)])
+    waiting = []
+
+    def quantise_waiting():
+        for w in waiting:
+            step("V", ("Q", w[0], w[1]), [("I", w[0], w[1])])
+        waiting.clear()
+
+    def chunk(grp, g):
+        if INTERLEAVE[grp][g] == "V":
+            interleave(grp, g)
+        quantise_waiting()
+        waiting.append((grp, g))
+
+    for g in range(PASSES):
+        chunk("k", g)
+        if g == 0:
+            step("V", ("tab2", "", 0), [("sin", "", 0)])
+        chunk("q0", g)
+    for i in range(PASSES):
+        step("V", ("X", "x", i), [("C", "x", i)])
+        chunk("q1", i)
+        chunk("v", i)
+    step("V", ("X", "x", 3), [("C", "x", 3)])
+    quantise_waiting()
+
+    banks = [(grp, m) for grp in ROPE_GROUPS for m in range(8)]
+    order = []
+    for n in range(32):
+        order.append(banks[n])
+        if n >= 16 and n % 2 == 0:
+            order.append(("v", (n - 16) // 2))
+    for grp, m in order:
+        step("P", ("MM", grp, m), [("Q", grp, g) for g in range(PASSES)] + [("X", "x", m // 2)])
+
+    def passed(n):
+        step("S", ("PA", banks[n][0], banks[n][1]), [("MM", banks[n][0], banks[n][1])])
+
+    done = 0
+    for j in range(2 * PASSES):
+        if j % 2 == 0:
+            widen(LATE, j // 2)
+        else:
+            interleave(LATE, j // 2)
+        while done < (5 * (j + 1)) // 2:
+            passed(done)
+            done += 1
+    for m in range(8):
+        passed(done)
+        passed(done + 1)
+        done += 2
+        step("S", ("VC", "v", m), [("MM", "v", m)])
+    passed(done)
+
+    for n in range(32):
+        grp, m = banks[n]
+        step("V", ("MU", grp, m), [("MM", grp, m), ("tab2", "", 0)])
+        step("G", ("AD", grp, m), [("MU", grp, m)])
+        if n % 6 == 0 and 0 < n <= 6 * PASSES:
+            step("V", ("Q", LATE, n // 6 - 1), [("I", LATE, n // 6 - 1)])
+    for grp, m in order:
+        if grp == "v":
+            step("D", ("ST", grp, m), [("VC", grp, m)])
+        else:
+            step("D", ("ST", grp, m), [("AD", grp, m), ("PA", grp, m)])
+
+    def ring(bufs, taken):
+        for n in range(bufs, len(taken)):
+            needs[taken[n][0]] = needs[taken[n][0]] + taken[n - bufs][1]
+
+    ring(WIDE_BUFS, [(s, [("I", s[1], s[2])]) for s in lists["S"] if s[0] == "W"])
+    for engine in ("S", "V"):
+        ring(WG_BUFS, [(s, [("Q", s[1], s[2])]) for s in lists[engine] if s[0] == "I"])
+    ring(XG_BUFS // PASSES, [(s, [("X", s[1], s[2])]) for s in lists["S"] if s[0] == "C"])
+    ring(Z_BUFS, [(s, [("AD", s[1], s[2])]) for s in lists["V"] if s[0] == "MU"])
+    ring(O_BUFS, [(s, [("ST", s[1], s[2])]) for s in lists["P"] if s[0] == "MM"])
+    in_psum = []
+    for s in lists["P"]:
+        if s[0] == "T":
+            in_psum.extend([(s, [("C", s[1], s[2])])] * PASSES)
+        elif s[1] == "v":
+            in_psum.append((s, [("VC", s[1], s[2])]))
+        else:
+            in_psum.append((s, [("MU", s[1], s[2]), ("PA", s[1], s[2])]))
+    ring(8, in_psum)
+    return lists, needs
+
+
+def one_text(lists, needs):
+    place = {"D": 0, "G": 0, "P": 0, "S": 0, "V": 0}
+    written = set()
+    text = []
+    moved = True
+    while moved:
+        moved = False
+        for engine in ("D", "G", "P", "S", "V"):
+            while place[engine] < len(lists[engine]) and all(b in written for b in needs[lists[engine][place[engine]]]):
+                name = lists[engine][place[engine]]
+                text.append((engine, name))
+                written.add(name)
+                place[engine] += 1
+                moved = True
+    assert len(text) == sum(len(lists[engine]) for engine in ("D", "G", "P", "S", "V"))
+    return text
 
 
 def tile_phi4miniattention_pa_kernel(tc, hidden_states, Wq_bytes, Wq_scale, Wk, Wv, out_0, out_1, out_2):
     nc = tc.nc
     with ExitStack() as ctx:
         keep = ctx.enter_context(tc.tile_pool(name="keep", bufs=1))
-        stage = ctx.enter_context(tc.tile_pool(name="stage", bufs=3))
-        work = ctx.enter_context(tc.tile_pool(name="work", bufs=4))
+        stage = ctx.enter_context(tc.tile_pool(name="stage", bufs=WIDE_BUFS))
+        work = ctx.enter_context(tc.tile_pool(name="work", bufs=O_BUFS))
         psum = ctx.enter_context(tc.psum_pool(name="psum", bufs=8))
+        ctx.enter_context(tc.manual_schedule())
 
         hs = hidden_states.rearrange("b s k -> (b s) k")
         wq_v = Wq_bytes.rearrange("(g p t) h d -> g p t (h d)", p=P, t=4)
-        wk_v = Wk.rearrange("(g p t) h d -> g p t (h d)", p=P, t=4)
-        wv_v = Wv.rearrange("(g p t) h d -> g p t (h d)", p=P, t=4)
-
-        sc = keep.tile([P, PASSES, 4], F32, name="sc")
-        nc.sync.dma_start(out=sc[:], in_=Wq_scale.rearrange("(g p t) a b -> p g (t a b)", p=P, t=4))
-
-        x_sb = []
-        for m in range(8):
-            x_t = keep.tile([P, K], BF16, name="x%d" % m)
-            x_sb.append(x_t)
-        wq_bytes_sb = {}
-        for cq in range(3):
-            for g in range(PASSES):
-                b_t = keep.tile([P, 4, NB], U8, name="wqbytes%d_%d" % (cq, g))
-                wq_bytes_sb[(cq, g)] = b_t
-        raw = {}
-        for grp in ("k", "v"):
-            for g in range(PASSES):
-                r_t = keep.tile([P, 4, NB], BF16, name="raw%s%d" % (grp, g))
-                raw[(grp, g)] = r_t
-
-        def load_x(m):
-            nc.sync.dma_start(out=x_sb[m][:], in_=hs[P * m:P * (m + 1), :])
-
-        def load_wq(cq, g):
-            nc.sync.dma_start(out=wq_bytes_sb[(cq, g)][:], in_=wq_v[g][:, :, NB * cq:NB * (cq + 1)])
-
-        load_wq(0, 0)
-        load_x(0)
-        load_x(1)
-        load_wq(0, 1)
-        load_x(2)
-        load_x(3)
-        load_wq(0, 2)
-        for m in range(4, 8):
-            load_x(m)
-        for cq in (1, 2):
-            for g in range(PASSES):
-                load_wq(cq, g)
-        for g in range(PASSES):
-            nc.sync.dma_start(out=raw[("k", g)][:], in_=wk_v[g])
-        for g in range(PASSES):
-            nc.sync.dma_start(out=raw[("v", g)][:], in_=wv_v[g])
-
-        zero1 = keep.tile([P, 1], F32, name="zero1")
-        nc.gpsimd.memset(zero1[:], 0.0)
-        warm = keep.tile([P, 1], F32, name="warm")
-        nc.scalar.activation(out=warm[:], in_=zero1[:], func=ACT.Sin)
-
-        pos = keep.tile([P, 4], F32, name="pos")
-        nc.gpsimd.iota(pos[:], pattern=[[P, 4]], base=0, channel_multiplier=1, allow_small_or_imprecise_dtypes=True)
-        ident = keep.tile([P, P], F32, name="ident")
-        make_identity(nc, ident[:])
-
-        with tc.high_priority():
-            theta = keep.tile([P, 4, HALF], F32, name="theta")
-            nc.vector.tensor_copy(out=theta[:, :, 0:1], in_=pos[:].unsqueeze(2))
-            for s in (1, 2, 4, 8, 16):
-                nc.vector.tensor_scalar(out=theta[:, :, s:2 * s], in0=theta[:, :, 0:s], scalar1=BASE ** (-s / 48.0), scalar2=None, op0=ALU.mult)
-            nc.vector.tensor_scalar(out=theta[:, :, 32:48], in0=theta[:, :, 0:16], scalar1=BASE ** (-32 / 48.0), scalar2=None, op0=ALU.mult)
-            turns_i = keep.tile([P, 4, HALF], I32, name="turns_i")
-            nc.vector.tensor_scalar(out=turns_i[:], in0=theta[:], scalar1=1.0 / (2.0 * math.pi), scalar2=None, op0=ALU.mult)
-            turns = keep.tile([P, 4, HALF], F32, name="turns")
-            nc.vector.tensor_copy(out=turns[:], in_=turns_i[:])
-            c_hi = 6.28125
-            c_lo = 2.0 * math.pi - c_hi
-            red = keep.tile([P, 4, HALF], F32, name="red")
-            nc.vector.scalar_tensor_tensor(out=red[:], in0=turns[:], scalar=-c_hi, in1=theta[:], op0=ALU.mult, op1=ALU.add)
-            args = keep.tile([P, 2, 4, HALF], F32, name="args")
-            nc.vector.scalar_tensor_tensor(out=args[:, 0], in0=turns[:], scalar=-c_lo, in1=red[:], op0=ALU.mult, op1=ALU.add)
-            nc.vector.tensor_scalar(out=args[:, 1], in0=args[:, 0], scalar1=-0.5 * math.pi, scalar2=None, op0=ALU.add)
-            halfsin = keep.tile([P, 2, 4, HALF], F32, name="halfsin")
-            nc.scalar.activation(out=halfsin[:], in_=args[:], func=ACT.Sin, scale=0.5)
-            sq = keep.tile([P, 2, 4, HALF], F32, name="sq")
-            nc.vector.tensor_tensor(out=sq[:], in0=halfsin[:], in1=halfsin[:], op=ALU.mult)
-            rot = keep.tile([P, 4, 2, 2, HALF], F32, name="rot")
-            nc.vector.tensor_scalar(out=rot[:, :, 0, 0, :], in0=sq[:, 0], scalar1=-2.0, scalar2=1.0, op0=ALU.mult, op1=ALU.add)
-            nc.vector.tensor_scalar(out=rot[:, :, 1, 1, :], in0=sq[:, 0], scalar1=-2.0, scalar2=1.0, op0=ALU.mult, op1=ALU.add)
-            nc.vector.tensor_scalar(out=rot[:, :, 1, 0, :], in0=sq[:, 1], scalar1=-2.0, scalar2=1.0, op0=ALU.mult, op1=ALU.add)
-            nc.vector.tensor_scalar(out=rot[:, :, 0, 1, :], in0=sq[:, 1], scalar1=2.0, scalar2=-1.0, op0=ALU.mult, op1=ALU.add)
-
-        xg = []
-        xc = []
-        xs = []
-        for g in range(PASSES):
-            xg_t = keep.tile([P, 4 * TOKENS], BF16, name="xg%d" % g, align_bytes=64)
-            xc_t = keep.tile([P, TOKENS], U32, name="xc%d" % g, align_bytes=64)
-            xs_t = keep.tile([P, TOKENS], U8, name="xs%d" % g, align_bytes=64)
-            xg.append(xg_t)
-            xc.append(xc_t)
-            xs.append(xs_t)
-        for i in range(4):
-            for g in range(PASSES):
-                xt = psum.tile([P, 2, 2, P], F32, name="xt", tag="bank")
-                for c in range(2):
-                    words = x_sb[2 * i + c][:].bitcast(F32)
-                    for u in range(2):
-                        nc.tensor.transpose(xt[:, c, u, :], words[:, 256 * g + u:256 * (g + 1):2], ident[:])
-                dst = xg[g][:].bitcast(F32)[:, 512 * i:512 * (i + 1)].rearrange("p (c r u) -> p c r u", c=2, u=2)
-                nc.scalar.copy(out=dst, in_=xt[:].rearrange("p c u r -> p c r u"))
-                nc.vector.quantize_mx(
-                    out=xc[g][:, 256 * i:256 * (i + 1)].bitcast(FP8X4),
-                    scales=xs[g][:, 256 * i:256 * (i + 1)],
-                    in_=xg[g][:, 1024 * i:1024 * (i + 1)],
-                )
-
+        w_dram = {
+            "k": Wk.rearrange("(g p t) h d -> g p t (h d)", p=P, t=4),
+            "v": Wv.rearrange("(g p t) h d -> g p t (h d)", p=P, t=4),
+        }
         outs = {
             "q0": out_0.rearrange("b s h d -> (b s) (h d)")[:, 0:NB],
             "q1": out_0.rearrange("b s h d -> (b s) (h d)")[:, NB:2 * NB],
@@ -155,79 +211,214 @@ def tile_phi4miniattention_pa_kernel(tc, hidden_states, Wq_bytes, Wq_scale, Wk, 
             "k": out_1.rearrange("b s h d -> (b s) (h d)"),
             "v": out_2.rearrange("b s h d -> (b s) (h d)"),
         }
-        waiting = {}
 
-        def finish_bank():
-            if "bank" in waiting:
-                p_out, p_in0, p_in1, p_dram, p_tile = waiting["bank"]
-                nc.vector.tensor_tensor(out=p_out, in0=p_in0, in1=p_in1, op=ALU.add)
-                nc.sync.dma_start(out=p_dram, in_=p_tile)
-                waiting.clear()
-
-        for grp in GROUPS:
-            wc = keep.tile([P, PASSES, NB], U32, name="wc_" + grp, align_bytes=64)
-            ws = keep.tile([P, PASSES, NB], U8, name="ws_" + grp, align_bytes=64)
+        sc = keep.tile([P, PASSES, 4], F32, name="sc")
+        x_sb = []
+        for m in range(8):
+            x_t = keep.tile([P, K], BF16, name="x%d" % m)
+            x_sb.append(x_t)
+        wq_bytes_sb = {}
+        for grp in ("q0", "q1", "q2"):
             for g in range(PASSES):
-                if grp in ("k", "v"):
-                    src = raw[(grp, g)]
-                else:
-                    cq = ("q0", "q1", "q2").index(grp)
-                    src = stage.tile([P, 4, NB], BF16, name="wide", tag="wide")
-                    for t in range(4):
-                        nc.scalar.activation(
-                            out=src[:, t, :],
-                            in_=wq_bytes_sb[(cq, g)][:, t, :].bitcast(FP8),
-                            func=ACT.Copy,
-                            scale=sc[:, g, t:t + 1],
-                        )
-                wg = stage.tile([P, NB, 4], BF16, name="wg", tag="wg", align_bytes=64)
-                if INTERLEAVE[grp][g] == "v":
-                    nc.vector.tensor_copy(out=wg[:], in_=src[:].rearrange("p t n -> p n t"))
-                elif INTERLEAVE[grp][g] == "a":
-                    nc.any.tensor_copy(out=wg[:], in_=src[:].rearrange("p t n -> p n t"))
-                else:
-                    nc.scalar.copy(out=wg[:], in_=src[:].rearrange("p t n -> p n t"))
+                b_t = keep.tile([P, 4, NB], U8, name="wqbytes%s_%d" % (grp, g))
+                wq_bytes_sb[(grp, g)] = b_t
+        planes = {}
+        for grp in ("k", "v"):
+            for g in range(PASSES):
+                r_t = keep.tile([P, 4, NB], BF16, name="raw%s%d" % (grp, g))
+                planes[(grp, g)] = r_t
+        xc = []
+        xs = []
+        for g in range(PASSES):
+            xc_t = keep.tile([P, TOKENS], U32, name="xc%d" % g, align_bytes=64)
+            xs_t = keep.tile([P, TOKENS], U8, name="xs%d" % g, align_bytes=64)
+            xc.append(xc_t)
+            xs.append(xs_t)
+        wc = {}
+        ws = {}
+        for grp in ("k", "q0", "q1", "q2", "v"):
+            wc_t = keep.tile([P, PASSES, NB], U32, name="wc_" + grp, align_bytes=64)
+            ws_t = keep.tile([P, PASSES, NB], U8, name="ws_" + grp, align_bytes=64)
+            wc[grp] = wc_t
+            ws[grp] = ws_t
+        zero1 = keep.tile([P, 1], F32, name="zero1")
+        warm = keep.tile([P, 1], F32, name="warm")
+        pos = keep.tile([P, 4], F32, name="pos")
+        ident = keep.tile([P, P], F32, name="ident")
+        theta = keep.tile([P, 4, HALF], F32, name="theta")
+        turns_i = keep.tile([P, 4, HALF], I32, name="turns_i")
+        turns = keep.tile([P, 4, HALF], F32, name="turns")
+        red = keep.tile([P, 4, HALF], F32, name="red")
+        args = keep.tile([P, 2, 4, HALF], F32, name="args")
+        halfsin = keep.tile([P, 2, 4, HALF], F32, name="halfsin")
+        sq = keep.tile([P, 2, 4, HALF], F32, name="sq")
+        rot = keep.tile([P, 4, 2, 2, HALF], F32, name="rot")
+        live = {}
+
+        def load(grp, g):
+            if grp == "sc":
+                nc.sync.dma_start(out=sc[:], in_=Wq_scale.rearrange("(g p t) a b -> p g (t a b)", p=P, t=4))
+            elif grp == "x":
+                nc.sync.dma_start(out=x_sb[g][:], in_=hs[P * g:P * (g + 1), :])
+            elif grp in ("k", "v"):
+                nc.sync.dma_start(out=planes[(grp, g)][:], in_=w_dram[grp][g])
+            else:
+                cq = ("q0", "q1", "q2").index(grp)
+                nc.sync.dma_start(out=wq_bytes_sb[(grp, g)][:], in_=wq_v[g][:, :, NB * cq:NB * (cq + 1)])
+
+        def constants():
+            nc.gpsimd.memset(zero1[:], 0.0)
+            nc.gpsimd.iota(pos[:], pattern=[[P, 4]], base=0, channel_multiplier=1, allow_small_or_imprecise_dtypes=True)
+            make_identity(nc, ident[:])
+
+        def table_angles():
+            nc.vector.tensor_copy(out=theta[:, :, 0:1], in_=pos[:].unsqueeze(2))
+            for s in (1, 2, 4, 8, 16):
+                nc.vector.tensor_scalar(out=theta[:, :, s:2 * s], in0=theta[:, :, 0:s], scalar1=BASE ** (-s / 48.0), scalar2=None, op0=ALU.mult)
+            nc.vector.tensor_scalar(out=theta[:, :, 32:48], in0=theta[:, :, 0:16], scalar1=BASE ** (-32 / 48.0), scalar2=None, op0=ALU.mult)
+            nc.vector.tensor_scalar(out=turns_i[:], in0=theta[:], scalar1=1.0 / (2.0 * math.pi), scalar2=None, op0=ALU.mult)
+            nc.vector.tensor_copy(out=turns[:], in_=turns_i[:])
+            c_hi = 6.28125
+            c_lo = 2.0 * math.pi - c_hi
+            nc.vector.scalar_tensor_tensor(out=red[:], in0=turns[:], scalar=-c_hi, in1=theta[:], op0=ALU.mult, op1=ALU.add)
+            nc.vector.scalar_tensor_tensor(out=args[:, 0], in0=turns[:], scalar=-c_lo, in1=red[:], op0=ALU.mult, op1=ALU.add)
+            nc.vector.tensor_scalar(out=args[:, 1], in0=args[:, 0], scalar1=-0.5 * math.pi, scalar2=None, op0=ALU.add)
+
+        def table_factors():
+            nc.vector.tensor_tensor(out=sq[:], in0=halfsin[:], in1=halfsin[:], op=ALU.mult)
+            nc.vector.tensor_scalar(out=rot[:, :, 0, 0, :], in0=sq[:, 0], scalar1=-2.0, scalar2=1.0, op0=ALU.mult, op1=ALU.add)
+            nc.vector.tensor_scalar(out=rot[:, :, 1, 1, :], in0=sq[:, 0], scalar1=-2.0, scalar2=1.0, op0=ALU.mult, op1=ALU.add)
+            nc.vector.tensor_scalar(out=rot[:, :, 1, 0, :], in0=sq[:, 1], scalar1=-2.0, scalar2=1.0, op0=ALU.mult, op1=ALU.add)
+            nc.vector.tensor_scalar(out=rot[:, :, 0, 1, :], in0=sq[:, 1], scalar1=2.0, scalar2=-1.0, op0=ALU.mult, op1=ALU.add)
+
+        def x_transposes(i):
+            for g in range(PASSES):
+                xt = psum.tile([P, 2, 2, P], F32, name="xt", tag="bank")
+                live[("xt", i, g)] = xt
+                for c in range(2):
+                    words = x_sb[2 * i + c][:].bitcast(F32)
+                    for u in range(2):
+                        nc.tensor.transpose(xt[:, c, u, :], words[:, 256 * g + u:256 * (g + 1):2], ident[:])
+
+        def x_copies(i):
+            for g in range(PASSES):
+                xg = stage.tile([P, 1024], BF16, name="xg", tag="xg", bufs=XG_BUFS, align_bytes=64)
+                live[("xg", i, g)] = xg
+                dst = xg[:].bitcast(F32).rearrange("p (c r u) -> p c r u", c=2, u=2)
+                nc.scalar.copy(out=dst, in_=live[("xt", i, g)][:].rearrange("p c u r -> p c r u"))
+
+        def x_quantise(i):
+            for g in range(PASSES):
                 nc.vector.quantize_mx(
-                    out=wc[:, g, :].bitcast(FP8X4),
-                    scales=ws[:, g, :],
-                    in_=wg[:].rearrange("p n t -> p (n t)"),
+                    out=xc[g][:, 256 * i:256 * (i + 1)].bitcast(FP8X4),
+                    scales=xs[g][:, 256 * i:256 * (i + 1)],
+                    in_=live[("xg", i, g)][:],
                 )
-            for m in range(8):
-                acc = psum.tile([P, NB], F32, name="acc", tag="bank")
-                for g in range(PASSES):
-                    nc.tensor.matmul_mx(
-                        out=acc[:],
-                        lhsT=xc[g][:, P * m:P * (m + 1)].bitcast(FP8X4),
-                        lhsT_scale=xs[g][:, P * m:P * (m + 1)],
-                        rhs=wc[:, g, :].bitcast(FP8X4),
-                        rhs_scale=ws[:, g, :],
-                        start=(g == 0),
-                        stop=(g == PASSES - 1),
-                    )
-                o = work.tile([P, NB], F32, name="o", tag="o")
-                if grp == "v":
-                    nc.any.tensor_copy(out=o[:], in_=acc[:])
-                else:
-                    a = m % 4
-                    y = acc[:].rearrange("p (h d) -> p h d", h=4)
-                    oh = o[:].rearrange("p (h d) -> p h d", h=4)
-                    z = work.tile([P, 4, 2, ROT], F32, name="z", tag="z")
-                    nc.vector.tensor_tensor(
-                        out=z[:],
-                        in0=y[:, :, 0:ROT].unsqueeze(2).to_broadcast([P, 4, 2, ROT]),
-                        in1=rot[:, a].rearrange("p r f j -> p r (f j)").unsqueeze(1).to_broadcast([P, 4, 2, ROT]),
-                        op=ALU.mult,
-                    )
-                    nc.scalar.copy(out=oh[:, :, ROT:HD], in_=y[:, :, ROT:HD])
-                    zv = z[:].rearrange("p h r (f j) -> p h r f j", f=2)
-                    finish_bank()
-                    waiting["bank"] = (
-                        oh[:, :, 0:ROT].rearrange("p h (r j) -> p h r j", r=2),
-                        zv[:, :, :, 0, :],
-                        zv[:, :, :, 1, :],
-                        outs[grp][P * m:P * (m + 1), :],
-                        o[:],
-                    )
-                if grp == "v":
-                    nc.sync.dma_start(out=outs[grp][P * m:P * (m + 1), :], in_=o[:])
-            finish_bank()
+
+        def widen(grp, g):
+            wide = stage.tile([P, 4, NB], BF16, name="wide", tag="wide")
+            planes[(grp, g)] = wide
+            for t in range(4):
+                nc.scalar.activation(
+                    out=wide[:, t, :],
+                    in_=wq_bytes_sb[(grp, g)][:, t, :].bitcast(FP8),
+                    func=ACT.Copy,
+                    scale=sc[:, g, t:t + 1],
+                )
+
+        def interleave(engine, grp, g):
+            wg = stage.tile([P, NB, 4], BF16, name="wg", tag="wg" + engine, bufs=WG_BUFS, align_bytes=64)
+            live[("wg", grp, g)] = wg
+            if engine == "V":
+                nc.vector.tensor_copy(out=wg[:], in_=planes[(grp, g)][:].rearrange("p t n -> p n t"))
+            else:
+                nc.scalar.copy(out=wg[:], in_=planes[(grp, g)][:].rearrange("p t n -> p n t"))
+
+        def quantise(grp, g):
+            nc.vector.quantize_mx(
+                out=wc[grp][:, g, :].bitcast(FP8X4),
+                scales=ws[grp][:, g, :],
+                in_=live[("wg", grp, g)][:].rearrange("p n t -> p (n t)"),
+            )
+
+        def products(grp, m):
+            acc = psum.tile([P, NB], F32, name="acc", tag="bank")
+            live[("acc", grp, m)] = acc
+            o = work.tile([P, NB], F32, name="o", tag="o")
+            live[("o", grp, m)] = o
+            for g in range(PASSES):
+                nc.tensor.matmul_mx(
+                    out=acc[:],
+                    lhsT=xc[g][:, P * m:P * (m + 1)].bitcast(FP8X4),
+                    lhsT_scale=xs[g][:, P * m:P * (m + 1)],
+                    rhs=wc[grp][:, g, :].bitcast(FP8X4),
+                    rhs_scale=ws[grp][:, g, :],
+                    start=(g == 0),
+                    stop=(g == PASSES - 1),
+                )
+
+        def rope_multiply(grp, m):
+            y = live[("acc", grp, m)][:].rearrange("p (h d) -> p h d", h=4)
+            z = work.tile([P, 4, 2, ROT], F32, name="z", tag="z", bufs=Z_BUFS)
+            live[("z", grp, m)] = z
+            nc.vector.tensor_tensor(
+                out=z[:],
+                in0=y[:, :, 0:ROT].unsqueeze(2).to_broadcast([P, 4, 2, ROT]),
+                in1=rot[:, m % 4].rearrange("p r f j -> p r (f j)").unsqueeze(1).to_broadcast([P, 4, 2, ROT]),
+                op=ALU.mult,
+            )
+
+        def pass_through(grp, m):
+            y = live[("acc", grp, m)][:].rearrange("p (h d) -> p h d", h=4)
+            oh = live[("o", grp, m)][:].rearrange("p (h d) -> p h d", h=4)
+            nc.scalar.copy(out=oh[:, :, ROT:HD], in_=y[:, :, ROT:HD])
+
+        def rope_add(grp, m):
+            oh = live[("o", grp, m)][:].rearrange("p (h d) -> p h d", h=4)
+            zv = live[("z", grp, m)][:].rearrange("p h r (f j) -> p h r f j", f=2)
+            nc.gpsimd.tensor_tensor(
+                out=oh[:, :, 0:ROT].rearrange("p h (r j) -> p h r j", r=2),
+                in0=zv[:, :, :, 0, :],
+                in1=zv[:, :, :, 1, :],
+                op=ALU.add,
+            )
+
+        lists, needs = engine_lists()
+        for engine, name in one_text(lists, needs):
+            kind, grp, n = name
+            if kind == "L":
+                load(grp, n)
+            elif kind == "const":
+                constants()
+            elif kind == "warm":
+                nc.scalar.activation(out=warm[:], in_=zero1[:], func=ACT.Sin)
+            elif kind == "tab1":
+                table_angles()
+            elif kind == "sin":
+                nc.scalar.activation(out=halfsin[:], in_=args[:], func=ACT.Sin, scale=0.5)
+            elif kind == "tab2":
+                table_factors()
+            elif kind == "T":
+                x_transposes(n)
+            elif kind == "C":
+                x_copies(n)
+            elif kind == "X":
+                x_quantise(n)
+            elif kind == "W":
+                widen(grp, n)
+            elif kind == "I":
+                interleave(engine, grp, n)
+            elif kind == "Q":
+                quantise(grp, n)
+            elif kind == "MM":
+                products(grp, n)
+            elif kind == "MU":
+                rope_multiply(grp, n)
+            elif kind == "PA":
+                pass_through(grp, n)
+            elif kind == "AD":
+                rope_add(grp, n)
+            elif kind == "VC":
+                nc.scalar.copy(out=live[("o", grp, n)][:], in_=live[("acc", grp, n)][:])
+            else:
+                nc.sync.dma_start(out=outs[grp][P * n:P * (n + 1), :], in_=live[("o", grp, n)][:])

@@ -27,13 +27,16 @@ NB = 512
 FLOPS = 2 * TOKENS * K * 2560
 
 ROPE_GROUPS = ("k", "q0", "q1", "q2")
-INTERLEAVE = {"k": "VVV", "q0": "VVV", "q1": "VSS", "q2": "SSS", "v": "VVV"}
-LATE = "q2"
+INTERLEAVE = {"k": "VVV", "q0": "VVV", "q1": "SSS", "q2": "SSS", "v": "VVV"}
+SINGLE_FROM = 30
+PASS_LEAD = 4
 WIDE_BUFS = 4
 WG_BUFS = 3
+WG_PAIR_BUFS = 2
 XG_BUFS = 6
-Z_BUFS = 6
-O_BUFS = 8
+XZ_BUFS = 4
+O_BUFS = 9
+OV_BUFS = 4
 
 
 def engine_lists():
@@ -59,15 +62,8 @@ def engine_lists():
     for g in range(PASSES):
         step("D", ("L", "k", g), [])
         step("D", ("L", "q0", g), [])
-    for g in range(PASSES):
-        step("D", ("L", "x", 2 * g), [])
-        step("D", ("L", "x", 2 * g + 1), [])
-        step("D", ("L", "q1", g), [])
-        step("D", ("L", "v", g), [])
-    step("D", ("L", "x", 6), [])
-    step("D", ("L", "x", 7), [])
-    for g in range(PASSES):
-        step("D", ("L", LATE, g), [])
+    for grp, g in (("x", 0), ("x", 1), ("q1", 0), ("x", 2), ("x", 3), ("v", 0), ("x", 4), ("x", 5), ("v", 1), ("x", 6), ("x", 7), ("q1", 1), ("v", 2), ("q1", 2), ("q2", 0), ("q2", 1), ("q2", 2)):
+        step("D", ("L", grp, g), [])
 
     step("G", ("const", "", 0), [])
     step("S", ("warm", "", 0), [("const", "", 0)])
@@ -78,12 +74,26 @@ def engine_lists():
         step("P", ("T", "x", i), [("L", "x", 2 * i), ("L", "x", 2 * i + 1), ("const", "", 0)])
     for g in range(PASSES):
         widen("q0", g)
-    for i in range(PASSES):
+    stream = []
+    for grp in ("q1", "q2"):
+        for g in range(PASSES):
+            stream.append(("W", grp, g))
+            stream.append(("I", grp, g))
+
+    def stream_quantise(grp, g):
+        c = (3 * ("q1", "q2").index(grp) + g) | 1
+        return ("Q", ("q1", "q2")[c // 3], c % 3)
+
+    def next_of_stream():
+        kind, grp, g = stream.pop(0)
+        if kind == "W":
+            widen(grp, g)
+        else:
+            interleave(grp, g)
+
+    for i in range(4):
         step("S", ("C", "x", i), [("T", "x", i)])
-        widen("q1", i)
-        if INTERLEAVE["q1"][i] == "S":
-            interleave("q1", i)
-    step("S", ("C", "x", 3), [("T", "x", 3)])
+        next_of_stream()
     waiting = []
 
     def quantise_waiting():
@@ -104,7 +114,6 @@ def engine_lists():
         chunk("q0", g)
     for i in range(PASSES):
         step("V", ("X", "x", i), [("C", "x", i)])
-        chunk("q1", i)
         chunk("v", i)
     step("V", ("X", "x", 3), [("C", "x", 3)])
     quantise_waiting()
@@ -113,52 +122,64 @@ def engine_lists():
     order = []
     for n in range(32):
         order.append(banks[n])
-        if n >= 16 and n % 2 == 0:
-            order.append(("v", (n - 16) // 2))
+        if 20 <= n < 28:
+            order.append(("v", n - 20))
     for grp, m in order:
-        step("P", ("MM", grp, m), [("Q", grp, g) for g in range(PASSES)] + [("X", "x", m // 2)])
+        if grp in ("q1", "q2"):
+            step("P", ("MM", grp, m), [stream_quantise(grp, g) for g in range(PASSES)] + [("X", "x", m // 2)])
+        else:
+            step("P", ("MM", grp, m), [("Q", grp, g) for g in range(PASSES)] + [("X", "x", m // 2)])
 
     def passed(n):
         step("S", ("PA", banks[n][0], banks[n][1]), [("MM", banks[n][0], banks[n][1])])
 
     done = 0
-    for j in range(2 * PASSES):
-        if j % 2 == 0:
-            widen(LATE, j // 2)
-        else:
-            interleave(LATE, j // 2)
-        while done < (5 * (j + 1)) // 2:
+    while done < PASS_LEAD:
+        passed(done)
+        done += 1
+    for j in range(len(stream)):
+        next_of_stream()
+        while done < PASS_LEAD + (5 * (j + 1)) // 2:
             passed(done)
             done += 1
     for m in range(8):
-        passed(done)
-        passed(done + 1)
-        done += 2
         step("S", ("VC", "v", m), [("MM", "v", m)])
-    passed(done)
+        passed(done)
+        done += 1
+    while done < 32:
+        passed(done)
+        done += 1
 
     for n in range(32):
         grp, m = banks[n]
         step("V", ("MU", grp, m), [("MM", grp, m), ("tab2", "", 0)])
-        step("G", ("AD", grp, m), [("MU", grp, m)])
-        if n % 6 == 0 and 0 < n <= 6 * PASSES:
-            step("V", ("Q", LATE, n // 6 - 1), [("I", LATE, n // 6 - 1)])
+        if n >= SINGLE_FROM:
+            step("G", ("AD", grp, m), [("MU", grp, m)])
+        elif m % 2 == 1:
+            step("G", ("AD", grp, m), [("MU", grp, m - 1), ("MU", grp, m)])
+        if n % 10 == 0 and n <= 20:
+            first, second = ((("q1", 0), ("q1", 1)), (("q1", 2), ("q2", 0)), (("q2", 1), ("q2", 2)))[n // 10]
+            step("V", ("Q", second[0], second[1]), [("I", first[0], first[1]), ("I", second[0], second[1])])
     for grp, m in order:
         if grp == "v":
             step("D", ("ST", grp, m), [("VC", grp, m)])
-        else:
+        elif banks.index((grp, m)) >= SINGLE_FROM:
             step("D", ("ST", grp, m), [("AD", grp, m), ("PA", grp, m)])
+        elif m % 2 == 1:
+            step("D", ("ST", grp, m), [("AD", grp, m), ("PA", grp, m - 1), ("PA", grp, m)])
 
     def ring(bufs, taken):
         for n in range(bufs, len(taken)):
             needs[taken[n][0]] = needs[taken[n][0]] + taken[n - bufs][1]
 
     ring(WIDE_BUFS, [(s, [("I", s[1], s[2])]) for s in lists["S"] if s[0] == "W"])
-    for engine in ("S", "V"):
-        ring(WG_BUFS, [(s, [("Q", s[1], s[2])]) for s in lists[engine] if s[0] == "I"])
+    ring(WG_BUFS, [(s, [("Q", s[1], s[2])]) for s in lists["V"] if s[0] == "I"])
+    ring(WG_PAIR_BUFS, [(s, [stream_quantise(s[1], s[2])]) for s in lists["S"] if s[0] == "I" and stream_quantise(s[1], s[2]) != ("Q", s[1], s[2])])
     ring(XG_BUFS // PASSES, [(s, [("X", s[1], s[2])]) for s in lists["S"] if s[0] == "C"])
-    ring(Z_BUFS, [(s, [("AD", s[1], s[2])]) for s in lists["V"] if s[0] == "MU"])
-    ring(O_BUFS, [(s, [("ST", s[1], s[2])]) for s in lists["P"] if s[0] == "MM"])
+    ring(XZ_BUFS, [(s, [("T", "x", s[2] // 2)]) for s in lists["D"] if s[0] == "L" and s[1] == "x" and s[2] % 2 == 0]
+         + [(s, [("AD", s[1], s[2] + 1)]) for s in lists["V"] if s[0] == "MU" and s[2] % 2 == 0])
+    ring(O_BUFS, [(s, [("ST", s[1], s[2] + 1)]) for s in lists["P"] if s[0] == "MM" and s[1] != "v" and s[2] % 2 == 0])
+    ring(OV_BUFS, [(s, [("ST", s[1], s[2])]) for s in lists["P"] if s[0] == "MM" and s[1] == "v"])
     in_psum = []
     for s in lists["P"]:
         if s[0] == "T":
@@ -213,10 +234,7 @@ def tile_phi4miniattention_pa_kernel(tc, hidden_states, Wq_bytes, Wq_scale, Wk, 
         }
 
         sc = keep.tile([P, PASSES, 4], F32, name="sc")
-        x_sb = []
-        for m in range(8):
-            x_t = keep.tile([P, K], BF16, name="x%d" % m)
-            x_sb.append(x_t)
+        x_sb = {}
         wq_bytes_sb = {}
         for grp in ("q0", "q1", "q2"):
             for g in range(PASSES):
@@ -236,11 +254,17 @@ def tile_phi4miniattention_pa_kernel(tc, hidden_states, Wq_bytes, Wq_scale, Wk, 
             xs.append(xs_t)
         wc = {}
         ws = {}
-        for grp in ("k", "q0", "q1", "q2", "v"):
+        for grp in ("k", "q0", "v"):
             wc_t = keep.tile([P, PASSES, NB], U32, name="wc_" + grp, align_bytes=64)
             ws_t = keep.tile([P, PASSES, NB], U8, name="ws_" + grp, align_bytes=64)
-            wc[grp] = wc_t
-            ws[grp] = ws_t
+            wc[grp] = wc_t[:]
+            ws[grp] = ws_t[:]
+        wc_stream = keep.tile([P, 2 * PASSES, NB], U32, name="wc_stream", align_bytes=64)
+        ws_stream = keep.tile([P, 2 * PASSES, NB], U8, name="ws_stream", align_bytes=64)
+        for grp in ("q1", "q2"):
+            first = PASSES * ("q1", "q2").index(grp)
+            wc[grp] = wc_stream[:, first:first + PASSES, :]
+            ws[grp] = ws_stream[:, first:first + PASSES, :]
         zero1 = keep.tile([P, 1], F32, name="zero1")
         warm = keep.tile([P, 1], F32, name="warm")
         pos = keep.tile([P, 4], F32, name="pos")
@@ -259,7 +283,10 @@ def tile_phi4miniattention_pa_kernel(tc, hidden_states, Wq_bytes, Wq_scale, Wk, 
             if grp == "sc":
                 nc.sync.dma_start(out=sc[:], in_=Wq_scale.rearrange("(g p t) a b -> p g (t a b)", p=P, t=4))
             elif grp == "x":
-                nc.sync.dma_start(out=x_sb[g][:], in_=hs[P * g:P * (g + 1), :])
+                if g % 2 == 0:
+                    x_t = work.tile([P, 2, K], BF16, name="x", tag="xz", bufs=XZ_BUFS)
+                    x_sb[g // 2] = x_t
+                nc.sync.dma_start(out=x_sb[g // 2][:, g % 2, :], in_=hs[P * g:P * (g + 1), :])
             elif grp in ("k", "v"):
                 nc.sync.dma_start(out=planes[(grp, g)][:], in_=w_dram[grp][g])
             else:
@@ -296,7 +323,7 @@ def tile_phi4miniattention_pa_kernel(tc, hidden_states, Wq_bytes, Wq_scale, Wk, 
                 xt = psum.tile([P, 2, 2, P], F32, name="xt", tag="bank")
                 live[("xt", i, g)] = xt
                 for c in range(2):
-                    words = x_sb[2 * i + c][:].bitcast(F32)
+                    words = x_sb[i][:, c, :].bitcast(F32)
                     for u in range(2):
                         nc.tensor.transpose(xt[:, c, u, :], words[:, 256 * g + u:256 * (g + 1):2], ident[:])
 
@@ -327,12 +354,25 @@ def tile_phi4miniattention_pa_kernel(tc, hidden_states, Wq_bytes, Wq_scale, Wk, 
                 )
 
         def interleave(engine, grp, g):
-            wg = stage.tile([P, NB, 4], BF16, name="wg", tag="wg" + engine, bufs=WG_BUFS, align_bytes=64)
-            live[("wg", grp, g)] = wg
+            src = planes[(grp, g)][:].rearrange("p t (c i) -> p c t i", i=4)
             if engine == "V":
-                nc.vector.tensor_copy(out=wg[:], in_=planes[(grp, g)][:].rearrange("p t n -> p n t"))
+                wg = stage.tile([P, NB, 4], BF16, name="wg", tag="wg", bufs=WG_BUFS, align_bytes=64)
+                live[("wg", grp, g)] = wg
+                nc.vector.tensor_copy(out=wg[:].rearrange("p (c i) t -> p c t i", i=4), in_=src)
             else:
-                nc.scalar.copy(out=wg[:], in_=planes[(grp, g)][:].rearrange("p t n -> p n t"))
+                c = PASSES * ("q1", "q2").index(grp) + g
+                if c % 2 == 0:
+                    wg2 = stage.tile([P, 2, NB, 4], BF16, name="wg2", tag="wg2", bufs=WG_PAIR_BUFS, align_bytes=64)
+                    live[("wg2", c // 2)] = wg2
+                nc.scalar.copy(out=live[("wg2", c // 2)][:, c % 2].rearrange("p (c i) t -> p c t i", i=4), in_=src)
+
+        def quantise_two(grp, g):
+            c = PASSES * ("q1", "q2").index(grp) + g
+            nc.vector.quantize_mx(
+                out=wc_stream[:, c - 1:c + 1, :].rearrange("p g n -> p (g n)").bitcast(FP8X4),
+                scales=ws_stream[:, c - 1:c + 1, :].rearrange("p g n -> p (g n)"),
+                in_=live[("wg2", c // 2)][:].rearrange("p b n t -> p (b n t)"),
+            )
 
         def quantise(grp, g):
             nc.vector.quantize_mx(
@@ -344,8 +384,13 @@ def tile_phi4miniattention_pa_kernel(tc, hidden_states, Wq_bytes, Wq_scale, Wk, 
         def products(grp, m):
             acc = psum.tile([P, NB], F32, name="acc", tag="bank")
             live[("acc", grp, m)] = acc
-            o = work.tile([P, NB], F32, name="o", tag="o")
-            live[("o", grp, m)] = o
+            if grp == "v":
+                ov = work.tile([P, 1, NB], F32, name="ov", tag="ov", bufs=OV_BUFS)
+                live[("o", grp, m)] = ov
+            elif m % 2 == 0:
+                o = work.tile([P, 2, NB], F32, name="o", tag="o")
+                live[("o", grp, m)] = o
+                live[("o", grp, m + 1)] = o
             for g in range(PASSES):
                 nc.tensor.matmul_mx(
                     out=acc[:],
@@ -359,10 +404,12 @@ def tile_phi4miniattention_pa_kernel(tc, hidden_states, Wq_bytes, Wq_scale, Wk, 
 
         def rope_multiply(grp, m):
             y = live[("acc", grp, m)][:].rearrange("p (h d) -> p h d", h=4)
-            z = work.tile([P, 4, 2, ROT], F32, name="z", tag="z", bufs=Z_BUFS)
-            live[("z", grp, m)] = z
+            if m % 2 == 0:
+                z = work.tile([P, 2, 4, 2, ROT], F32, name="z", tag="xz", bufs=XZ_BUFS)
+                live[("z", grp, m)] = z
+                live[("z", grp, m + 1)] = z
             nc.vector.tensor_tensor(
-                out=z[:],
+                out=live[("z", grp, m)][:, m % 2],
                 in0=y[:, :, 0:ROT].unsqueeze(2).to_broadcast([P, 4, 2, ROT]),
                 in1=rot[:, m % 4].rearrange("p r f j -> p r (f j)").unsqueeze(1).to_broadcast([P, 4, 2, ROT]),
                 op=ALU.mult,
@@ -370,12 +417,12 @@ def tile_phi4miniattention_pa_kernel(tc, hidden_states, Wq_bytes, Wq_scale, Wk, 
 
         def pass_through(grp, m):
             y = live[("acc", grp, m)][:].rearrange("p (h d) -> p h d", h=4)
-            oh = live[("o", grp, m)][:].rearrange("p (h d) -> p h d", h=4)
+            oh = live[("o", grp, m)][:, m % 2, :].rearrange("p (h d) -> p h d", h=4)
             nc.scalar.copy(out=oh[:, :, ROT:HD], in_=y[:, :, ROT:HD])
 
-        def rope_add(grp, m):
-            oh = live[("o", grp, m)][:].rearrange("p (h d) -> p h d", h=4)
-            zv = live[("z", grp, m)][:].rearrange("p h r (f j) -> p h r f j", f=2)
+        def rope_add(grp, m, first):
+            oh = live[("o", grp, m)][:, first % 2:m % 2 + 1, :].rearrange("p b (h d) -> p (b h) d", h=4)
+            zv = live[("z", grp, m)][:, first % 2:m % 2 + 1].rearrange("p b h r (f j) -> p (b h) r f j", f=2)
             nc.gpsimd.tensor_tensor(
                 out=oh[:, :, 0:ROT].rearrange("p h (r j) -> p h r j", r=2),
                 in0=zv[:, :, :, 0, :],
@@ -408,6 +455,8 @@ def tile_phi4miniattention_pa_kernel(tc, hidden_states, Wq_bytes, Wq_scale, Wk, 
                 widen(grp, n)
             elif kind == "I":
                 interleave(engine, grp, n)
+            elif kind == "Q" and grp in ("q1", "q2"):
+                quantise_two(grp, n)
             elif kind == "Q":
                 quantise(grp, n)
             elif kind == "MM":
@@ -416,9 +465,13 @@ def tile_phi4miniattention_pa_kernel(tc, hidden_states, Wq_bytes, Wq_scale, Wk, 
                 rope_multiply(grp, n)
             elif kind == "PA":
                 pass_through(grp, n)
+            elif kind == "AD" and ROPE_GROUPS.index(grp) * 8 + n >= SINGLE_FROM:
+                rope_add(grp, n, n)
             elif kind == "AD":
-                rope_add(grp, n)
+                rope_add(grp, n, n - 1)
             elif kind == "VC":
-                nc.scalar.copy(out=live[("o", grp, n)][:], in_=live[("acc", grp, n)][:])
+                nc.scalar.copy(out=live[("o", grp, n)][:, 0, :], in_=live[("acc", grp, n)][:])
+            elif grp == "v" or ROPE_GROUPS.index(grp) * 8 + n >= SINGLE_FROM:
+                nc.sync.dma_start(out=outs[grp][P * n:P * (n + 1), :], in_=live[("o", grp, n)][:, n % 2 if grp != "v" else 0, :])
             else:
-                nc.sync.dma_start(out=outs[grp][P * n:P * (n + 1), :], in_=live[("o", grp, n)][:])
+                nc.sync.dma_start(out=outs[grp][P * (n - 1):P * (n + 1), :].rearrange("(b p) c -> p b c", b=2), in_=live[("o", grp, n)][:])

@@ -107,11 +107,9 @@ def engine_lists():
         quantise_waiting()
         waiting.append((grp, g))
 
-    for g in range(PASSES):
-        chunk("k", g)
-        if g == 0:
-            step("V", ("tab2", "", 0), [("sin", "", 0)])
-        chunk("q0", g)
+    step("V", ("tab2", "", 0), [("sin", "", 0)])
+    for grp, g in (("k", 0), ("k", 1), ("q0", 0), ("k", 2), ("q0", 1), ("q0", 2)):
+        chunk(grp, g)
     for i in range(PASSES):
         step("V", ("X", "x", i), [("C", "x", i)])
         chunk("v", i)
@@ -153,13 +151,13 @@ def engine_lists():
     for n in range(32):
         grp, m = banks[n]
         step("V", ("MU", grp, m), [("MM", grp, m), ("tab2", "", 0)])
-        if n >= SINGLE_FROM:
-            step("G", ("AD", grp, m), [("MU", grp, m)])
-        elif m % 2 == 1:
+        if n < SINGLE_FROM and m % 2 == 1:
             step("G", ("AD", grp, m), [("MU", grp, m - 1), ("MU", grp, m)])
         if n % 10 == 0 and n <= 20:
             first, second = ((("q1", 0), ("q1", 1)), (("q1", 2), ("q2", 0)), (("q2", 1), ("q2", 2)))[n // 10]
             step("V", ("Q", second[0], second[1]), [("I", first[0], first[1]), ("I", second[0], second[1])])
+    for n in range(SINGLE_FROM, 32):
+        step("V", ("AD", banks[n][0], banks[n][1]), [("MU", banks[n][0], banks[n][1])])
     for grp, m in order:
         if grp == "v":
             step("D", ("ST", grp, m), [("VC", grp, m)])
@@ -420,10 +418,11 @@ def tile_phi4miniattention_pa_kernel(tc, hidden_states, Wq_bytes, Wq_scale, Wk, 
             oh = live[("o", grp, m)][:, m % 2, :].rearrange("p (h d) -> p h d", h=4)
             nc.scalar.copy(out=oh[:, :, ROT:HD], in_=y[:, :, ROT:HD])
 
-        def rope_add(grp, m, first):
+        def rope_add(engine, grp, m, first):
             oh = live[("o", grp, m)][:, first % 2:m % 2 + 1, :].rearrange("p b (h d) -> p (b h) d", h=4)
             zv = live[("z", grp, m)][:, first % 2:m % 2 + 1].rearrange("p b h r (f j) -> p (b h) r f j", f=2)
-            nc.gpsimd.tensor_tensor(
+            adder = nc.vector if engine == "V" else nc.gpsimd
+            adder.tensor_tensor(
                 out=oh[:, :, 0:ROT].rearrange("p h (r j) -> p h r j", r=2),
                 in0=zv[:, :, :, 0, :],
                 in1=zv[:, :, :, 1, :],
@@ -466,9 +465,9 @@ def tile_phi4miniattention_pa_kernel(tc, hidden_states, Wq_bytes, Wq_scale, Wk, 
             elif kind == "PA":
                 pass_through(grp, n)
             elif kind == "AD" and ROPE_GROUPS.index(grp) * 8 + n >= SINGLE_FROM:
-                rope_add(grp, n, n)
+                rope_add(engine, grp, n, n)
             elif kind == "AD":
-                rope_add(grp, n, n - 1)
+                rope_add(engine, grp, n, n - 1)
             elif kind == "VC":
                 nc.scalar.copy(out=live[("o", grp, n)][:, 0, :], in_=live[("acc", grp, n)][:])
             elif grp == "v" or ROPE_GROUPS.index(grp) * 8 + n >= SINGLE_FROM:

@@ -60,20 +60,21 @@ def engine_lists():
 
     step("D", ("L", "sc", 0), [])
     for g in range(PASSES):
-        step("D", ("L", "k", g), [])
         step("D", ("L", "q0", g), [])
+        step("D", ("L", "k", g), [])
     for grp, g in (("x", 0), ("x", 1), ("q1", 0), ("x", 2), ("x", 3), ("v", 0), ("x", 4), ("x", 5), ("v", 1), ("x", 6), ("x", 7), ("q1", 1), ("v", 2), ("q1", 2), ("q2", 0), ("q2", 1), ("q2", 2)):
         step("D", ("L", grp, g), [])
 
     step("G", ("const", "", 0), [])
     step("S", ("warm", "", 0), [("const", "", 0)])
     step("V", ("tab1", "", 0), [("const", "", 0)])
-    step("S", ("sin", "", 0), [("tab1", "", 0)])
 
     for i in range(4):
         step("P", ("T", "x", i), [("L", "x", 2 * i), ("L", "x", 2 * i + 1), ("const", "", 0)])
     for g in range(PASSES):
         widen("q0", g)
+        if g == 1:
+            step("S", ("sin", "", 0), [("tab1", "", 0)])
     stream = []
     for grp in ("q1", "q2"):
         for g in range(PASSES):
@@ -107,9 +108,9 @@ def engine_lists():
         quantise_waiting()
         waiting.append((grp, g))
 
-    step("V", ("tab2", "", 0), [("sin", "", 0)])
     for grp, g in (("k", 0), ("k", 1), ("q0", 0), ("k", 2), ("q0", 1), ("q0", 2)):
         chunk(grp, g)
+    step("V", ("tab2", "", 0), [("sin", "", 0)])
     for i in range(PASSES):
         step("V", ("X", "x", i), [("C", "x", i)])
         chunk("v", i)

@@ -35,7 +35,7 @@ WG_BUFS = 3
 WG_PAIR_BUFS = 2
 XG_BUFS = 6
 XZ_BUFS = 4
-O_BUFS = 9
+O_BUFS = 6
 OV_BUFS = 4
 
 
@@ -111,10 +111,11 @@ def engine_lists():
     for grp, g in (("k", 0), ("k", 1), ("q0", 0), ("k", 2), ("q0", 1), ("q0", 2)):
         chunk(grp, g)
     step("V", ("tab2", "", 0), [("sin", "", 0)])
-    for i in range(PASSES):
-        step("V", ("X", "x", i), [("C", "x", i)])
-        chunk("v", i)
-    step("V", ("X", "x", 3), [("C", "x", 3)])
+    chunk("v", 0)
+    step("V", ("X", "x", 1), [("C", "x", 0), ("C", "x", 1)])
+    chunk("v", 1)
+    chunk("v", 2)
+    step("V", ("X", "x", 3), [("C", "x", 2), ("C", "x", 3)])
     quantise_waiting()
 
     banks = [(grp, m) for grp in ROPE_GROUPS for m in range(8)]
@@ -125,9 +126,9 @@ def engine_lists():
             order.append(("v", n - 20))
     for grp, m in order:
         if grp in ("q1", "q2"):
-            step("P", ("MM", grp, m), [stream_quantise(grp, g) for g in range(PASSES)] + [("X", "x", m // 2)])
+            step("P", ("MM", grp, m), [stream_quantise(grp, g) for g in range(PASSES)] + [("X", "x", (m // 2) | 1)])
         else:
-            step("P", ("MM", grp, m), [("Q", grp, g) for g in range(PASSES)] + [("X", "x", m // 2)])
+            step("P", ("MM", grp, m), [("Q", grp, g) for g in range(PASSES)] + [("X", "x", (m // 2) | 1)])
 
     def passed(n):
         step("S", ("PA", banks[n][0], banks[n][1]), [("MM", banks[n][0], banks[n][1])])
@@ -174,7 +175,7 @@ def engine_lists():
     ring(WIDE_BUFS, [(s, [("I", s[1], s[2])]) for s in lists["S"] if s[0] == "W"])
     ring(WG_BUFS, [(s, [("Q", s[1], s[2])]) for s in lists["V"] if s[0] == "I"])
     ring(WG_PAIR_BUFS, [(s, [stream_quantise(s[1], s[2])]) for s in lists["S"] if s[0] == "I" and stream_quantise(s[1], s[2]) != ("Q", s[1], s[2])])
-    ring(XG_BUFS // PASSES, [(s, [("X", s[1], s[2])]) for s in lists["S"] if s[0] == "C"])
+    ring(XG_BUFS // PASSES, [(s, [("X", s[1], s[2] + 1)]) for s in lists["S"] if s[0] == "C" and s[2] % 2 == 0])
     ring(XZ_BUFS, [(s, [("T", "x", s[2] // 2)]) for s in lists["D"] if s[0] == "L" and s[1] == "x" and s[2] % 2 == 0]
          + [(s, [("AD", s[1], s[2] + 1)]) for s in lists["V"] if s[0] == "MU" and s[2] % 2 == 0])
     ring(O_BUFS, [(s, [("ST", s[1], s[2] + 1)]) for s in lists["P"] if s[0] == "MM" and s[1] != "v" and s[2] % 2 == 0])
@@ -328,17 +329,18 @@ def tile_phi4miniattention_pa_kernel(tc, hidden_states, Wq_bytes, Wq_scale, Wk, 
 
         def x_copies(i):
             for g in range(PASSES):
-                xg = stage.tile([P, 1024], BF16, name="xg", tag="xg", bufs=XG_BUFS, align_bytes=64)
-                live[("xg", i, g)] = xg
-                dst = xg[:].bitcast(F32).rearrange("p (c r u) -> p c r u", c=2, u=2)
+                if i % 2 == 0:
+                    xg = stage.tile([P, 2, 1024], BF16, name="xg", tag="xg", bufs=XG_BUFS, align_bytes=64)
+                    live[("xg", i // 2, g)] = xg
+                dst = live[("xg", i // 2, g)][:, i % 2, :].bitcast(F32).rearrange("p (c r u) -> p c r u", c=2, u=2)
                 nc.scalar.copy(out=dst, in_=live[("xt", i, g)][:].rearrange("p c u r -> p c r u"))
 
         def x_quantise(i):
             for g in range(PASSES):
                 nc.vector.quantize_mx(
-                    out=xc[g][:, 256 * i:256 * (i + 1)].bitcast(FP8X4),
-                    scales=xs[g][:, 256 * i:256 * (i + 1)],
-                    in_=live[("xg", i, g)][:],
+                    out=xc[g][:, 256 * (i - 1):256 * (i + 1)].bitcast(FP8X4),
+                    scales=xs[g][:, 256 * (i - 1):256 * (i + 1)],
+                    in_=live[("xg", i // 2, g)][:].rearrange("p b c -> p (b c)"),
                 )
 
         def widen(grp, g):

@@ -53,7 +53,7 @@ def engine_lists():
         return ("W", grp, g)
 
     def widen(grp, g):
-        step("S", ("W", grp, g), [("L", grp, g), ("L", "sc", 0)])
+        step("S", ("W", grp, g), [("L", "q0" if grp == "q0" else "qs", g), ("L", "sc", 0)])
 
     def interleave(grp, g):
         step(INTERLEAVE[grp][g], ("I", grp, g), [source(grp, g)])
@@ -62,7 +62,7 @@ def engine_lists():
     for g in range(PASSES):
         step("D", ("L", "q0", g), [])
         step("D", ("L", "k", g), [])
-    for grp, g in (("x", 0), ("x", 1), ("q1", 0), ("x", 2), ("x", 3), ("v", 0), ("x", 4), ("x", 5), ("v", 1), ("x", 6), ("x", 7), ("q1", 1), ("v", 2), ("q1", 2), ("q2", 0), ("q2", 1), ("q2", 2)):
+    for grp, g in (("x", 0), ("qs", 0), ("x", 1), ("v", 0), ("x", 2), ("v", 1), ("x", 3), ("qs", 1), ("v", 2), ("qs", 2)):
         step("D", ("L", grp, g), [])
 
     step("G", ("const", "", 0), [])
@@ -70,7 +70,7 @@ def engine_lists():
     step("V", ("tab1", "", 0), [("const", "", 0)])
 
     for i in range(4):
-        step("P", ("T", "x", i), [("L", "x", 2 * i), ("L", "x", 2 * i + 1), ("const", "", 0)])
+        step("P", ("T", "x", i), [("L", "x", i), ("const", "", 0)])
     for g in range(PASSES):
         widen("q0", g)
         if g == 1:
@@ -176,7 +176,7 @@ def engine_lists():
     ring(WG_BUFS, [(s, [("Q", s[1], s[2])]) for s in lists["V"] if s[0] == "I"])
     ring(WG_PAIR_BUFS, [(s, [stream_quantise(s[1], s[2])]) for s in lists["S"] if s[0] == "I" and stream_quantise(s[1], s[2]) != ("Q", s[1], s[2])])
     ring(XG_BUFS // PASSES, [(s, [("X", s[1], s[2] + 1)]) for s in lists["S"] if s[0] == "C" and s[2] % 2 == 0])
-    ring(XZ_BUFS, [(s, [("T", "x", s[2] // 2)]) for s in lists["D"] if s[0] == "L" and s[1] == "x" and s[2] % 2 == 0]
+    ring(XZ_BUFS, [(s, [("T", "x", s[2])]) for s in lists["D"] if s[0] == "L" and s[1] == "x"]
          + [(s, [("AD", s[1], s[2] + 1)]) for s in lists["V"] if s[0] == "MU" and s[2] % 2 == 0])
     ring(O_BUFS, [(s, [("ST", s[1], s[2] + 1)]) for s in lists["P"] if s[0] == "MM" and s[1] != "v" and s[2] % 2 == 0])
     ring(OV_BUFS, [(s, [("ST", s[1], s[2])]) for s in lists["P"] if s[0] == "MM" and s[1] == "v"])
@@ -236,10 +236,13 @@ def tile_phi4miniattention_pa_kernel(tc, hidden_states, Wq_bytes, Wq_scale, Wk, 
         sc = keep.tile([P, PASSES, 4], F32, name="sc")
         x_sb = {}
         wq_bytes_sb = {}
-        for grp in ("q0", "q1", "q2"):
-            for g in range(PASSES):
-                b_t = keep.tile([P, 4, NB], U8, name="wqbytes%s_%d" % (grp, g))
-                wq_bytes_sb[(grp, g)] = b_t
+        for g in range(PASSES):
+            b_t = keep.tile([P, 4, NB], U8, name="wqbytesq0_%d" % g)
+            wq_bytes_sb[("q0", g)] = b_t[:]
+            b2_t = keep.tile([P, 4, 2 * NB], U8, name="wqbytesqs_%d" % g)
+            wq_bytes_sb[("qs", g)] = b2_t[:]
+            wq_bytes_sb[("q1", g)] = b2_t[:, :, 0:NB]
+            wq_bytes_sb[("q2", g)] = b2_t[:, :, NB:2 * NB]
         planes = {}
         for grp in ("k", "v"):
             for g in range(PASSES):
@@ -283,15 +286,15 @@ def tile_phi4miniattention_pa_kernel(tc, hidden_states, Wq_bytes, Wq_scale, Wk, 
             if grp == "sc":
                 nc.sync.dma_start(out=sc[:], in_=Wq_scale.rearrange("(g p t) a b -> p g (t a b)", p=P, t=4))
             elif grp == "x":
-                if g % 2 == 0:
-                    x_t = work.tile([P, 2, K], BF16, name="x", tag="xz", bufs=XZ_BUFS)
-                    x_sb[g // 2] = x_t
-                nc.sync.dma_start(out=x_sb[g // 2][:, g % 2, :], in_=hs[P * g:P * (g + 1), :])
+                x_t = work.tile([P, 2, K], BF16, name="x", tag="xz", bufs=XZ_BUFS)
+                x_sb[g] = x_t
+                nc.sync.dma_start(out=x_t[:], in_=hs[2 * P * g:2 * P * (g + 1), :].rearrange("(b p) k -> p b k", b=2))
             elif grp in ("k", "v"):
                 nc.sync.dma_start(out=planes[(grp, g)][:], in_=w_dram[grp][g])
+            elif grp == "q0":
+                nc.sync.dma_start(out=wq_bytes_sb[(grp, g)], in_=wq_v[g][:, :, 0:NB])
             else:
-                cq = ("q0", "q1", "q2").index(grp)
-                nc.sync.dma_start(out=wq_bytes_sb[(grp, g)][:], in_=wq_v[g][:, :, NB * cq:NB * (cq + 1)])
+                nc.sync.dma_start(out=wq_bytes_sb[(grp, g)], in_=wq_v[g][:, :, NB:3 * NB])
 
         def constants():
             nc.gpsimd.memset(zero1[:], 0.0)

@@ -27,163 +27,151 @@ NB = 512
 FLOPS = 2 * TOKENS * K * 2560
 
 ROPE_GROUPS = ("k", "q0", "q1", "q2")
-INTERLEAVE = {"k": "VVV", "q0": "VVV", "q1": "SSS", "q2": "SSS", "v": "VVV"}
 SINGLE_FROM = 30
-PASS_LEAD = 4
 WIDE_BUFS = 4
-WG_BUFS = 3
-WG_PAIR_BUFS = 2
+RAW_BUFS = 3
+WG_BUFS = 4
+WG_LATE_BUFS = 1
+WG_PAIR_BUFS = 3
 XG_BUFS = 6
 XZ_BUFS = 4
 O_BUFS = 6
 OV_BUFS = 4
 
+BANKS = [(grp, m) for grp in ROPE_GROUPS for m in range(8)]
+LOADS = "L sc 0,L q0 0,L k 0,L qs 0,L q0 1,L k 1,L q0 2,L k 2,L x 0,L x 1,L x 2,L x 3,L v 0,L v 1,L qs 1,L v 2,L qs 2"
+SCALAR_FIRST = "W q0 0,W q1 0,sin . 0,W q0 1,W q0 2,C x 0,C x 1,C x 2,C x 3"
+VECTOR_FIRST = "I k 0,Q k 0,I q0 0,I k 1,Q q0 0,I k 2,Q k 1,I q0 1,Q k 2,I q0 2,Q q0 1,I q1 0,Q q0 2,X x 1,I v 0,X x 3,Q v 0,I v 1"
+VECTOR_BETWEEN = {0: "Q v 1", 1: "Q v 2", 5: "I q1 2", 9: "Q q1 1", 11: "Q q2 0", 21: "Q q2 2"}
+SCALAR_STREAM = "W q1 1,I v 2,W q1 2,W q2 0,I q1 1,I q2 0,W q2 1,I q2 1,W q2 2,I q2 2"
+COPIES, STEPS = 5, 2
+V_AFTER = range(12, 28, 2)
+TENSOR_INTERLEAVE = ()
+
+
+def names(text):
+    out = []
+    for word in text.split(","):
+        kind, grp, n = word.split(" ")
+        out.append((kind, grp, int(n)))
+    return out
+
+
+def pair_of(grp, g):
+    c = PASSES * ("q1", "q2").index(grp) + g
+    last = c | 1
+    return c // 2, c % 2, ("Q", ("q1", "q2")[last // PASSES], last % PASSES)
+
+
+def quantise_step(grp, g):
+    if grp in ("q1", "q2"):
+        return pair_of(grp, g)[2]
+    return ("Q", grp, g)
+
+
+def add_step(grp, m):
+    if BANKS.index((grp, m)) >= SINGLE_FROM:
+        return ("AD", grp, m)
+    return ("AD", grp, m | 1)
+
+
+def store_step(grp, m):
+    if grp == "v" or BANKS.index((grp, m)) >= SINGLE_FROM:
+        return ("ST", grp, m)
+    return ("ST", grp, m | 1)
+
 
 def engine_lists():
-    lists = {"D": [], "G": [], "P": [], "S": [], "V": []}
-    needs = {}
-
-    def step(engine, name, before):
-        lists[engine].append(name)
-        needs[name] = before
-
-    def source(grp, g):
-        if grp in ("k", "v"):
-            return ("L", grp, g)
-        return ("W", grp, g)
-
-    def widen(grp, g):
-        step("S", ("W", grp, g), [("L", "q0" if grp == "q0" else "qs", g), ("L", "sc", 0)])
-
-    def interleave(grp, g):
-        step(INTERLEAVE[grp][g], ("I", grp, g), [source(grp, g)])
-
-    step("D", ("L", "sc", 0), [])
-    for g in range(PASSES):
-        step("D", ("L", "q0", g), [])
-        step("D", ("L", "k", g), [])
-    for grp, g in (("x", 0), ("qs", 0), ("x", 1), ("v", 0), ("x", 2), ("v", 1), ("x", 3), ("qs", 1), ("v", 2), ("qs", 2)):
-        step("D", ("L", grp, g), [])
-
-    step("G", ("const", "", 0), [])
-    step("S", ("warm", "", 0), [("const", "", 0)])
-    step("V", ("tab1", "", 0), [("const", "", 0)])
-
-    for i in range(4):
-        step("P", ("T", "x", i), [("L", "x", i), ("const", "", 0)])
-    for g in range(PASSES):
-        widen("q0", g)
-        if g == 1:
-            step("S", ("sin", "", 0), [("tab1", "", 0)])
-    stream = []
-    for grp in ("q1", "q2"):
-        for g in range(PASSES):
-            stream.append(("W", grp, g))
-            stream.append(("I", grp, g))
-
-    def stream_quantise(grp, g):
-        c = (3 * ("q1", "q2").index(grp) + g) | 1
-        return ("Q", ("q1", "q2")[c // 3], c % 3)
-
-    def next_of_stream():
-        kind, grp, g = stream.pop(0)
-        if kind == "W":
-            widen(grp, g)
-        else:
-            interleave(grp, g)
-
-    for i in range(4):
-        step("S", ("C", "x", i), [("T", "x", i)])
-        next_of_stream()
-    waiting = []
-
-    def quantise_waiting():
-        for w in waiting:
-            step("V", ("Q", w[0], w[1]), [("I", w[0], w[1])])
-        waiting.clear()
-
-    def chunk(grp, g):
-        if INTERLEAVE[grp][g] == "V":
-            interleave(grp, g)
-        quantise_waiting()
-        waiting.append((grp, g))
-
-    for grp, g in (("k", 0), ("k", 1), ("q0", 0), ("k", 2), ("q0", 1), ("q0", 2)):
-        chunk(grp, g)
-    step("V", ("tab2", "", 0), [("sin", "", 0)])
-    chunk("v", 0)
-    step("V", ("X", "x", 1), [("C", "x", 0), ("C", "x", 1)])
-    chunk("v", 1)
-    chunk("v", 2)
-    step("V", ("X", "x", 3), [("C", "x", 2), ("C", "x", 3)])
-    quantise_waiting()
-
-    banks = [(grp, m) for grp in ROPE_GROUPS for m in range(8)]
-    order = []
+    lists = {"D": names(LOADS), "G": [("const", ".", 0)], "P": [("T", "x", i) for i in range(4)], "S": [("warm", ".", 0)] + names(SCALAR_FIRST), "V": [("tab", ".", 0)] + names(VECTOR_FIRST)}
+    copies = []
+    v_banks = 0
     for n in range(32):
-        order.append(banks[n])
-        if 20 <= n < 28:
-            order.append(("v", n - 20))
-    for grp, m in order:
-        if grp in ("q1", "q2"):
-            step("P", ("MM", grp, m), [stream_quantise(grp, g) for g in range(PASSES)] + [("X", "x", (m // 2) | 1)])
-        else:
-            step("P", ("MM", grp, m), [("Q", grp, g) for g in range(PASSES)] + [("X", "x", (m // 2) | 1)])
-
-    def passed(n):
-        step("S", ("PA", banks[n][0], banks[n][1]), [("MM", banks[n][0], banks[n][1])])
-
-    done = 0
-    while done < PASS_LEAD:
-        passed(done)
-        done += 1
-    for j in range(len(stream)):
-        next_of_stream()
-        while done < PASS_LEAD + (5 * (j + 1)) // 2:
-            passed(done)
-            done += 1
-    for m in range(8):
-        step("S", ("VC", "v", m), [("MM", "v", m)])
-        passed(done)
-        done += 1
-    while done < 32:
-        passed(done)
-        done += 1
-
-    for n in range(32):
-        grp, m = banks[n]
-        step("V", ("MU", grp, m), [("MM", grp, m), ("tab2", "", 0)])
+        grp, m = BANKS[n]
+        lists["P"].append(("MM", grp, m))
+        copies.append(("PA", grp, m))
+        if n in V_AFTER:
+            lists["P"].append(("MM", "v", v_banks))
+            copies.append(("VC", "v", v_banks))
+            v_banks += 1
+        lists["V"].append(("MU", grp, m))
+        if n in VECTOR_BETWEEN:
+            lists["V"].extend(names(VECTOR_BETWEEN[n]))
         if n < SINGLE_FROM and m % 2 == 1:
-            step("G", ("AD", grp, m), [("MU", grp, m - 1), ("MU", grp, m)])
-        if n % 10 == 0 and n <= 20:
-            first, second = ((("q1", 0), ("q1", 1)), (("q1", 2), ("q2", 0)), (("q2", 1), ("q2", 2)))[n // 10]
-            step("V", ("Q", second[0], second[1]), [("I", first[0], first[1]), ("I", second[0], second[1])])
+            lists["G"].append(("AD", grp, m))
     for n in range(SINGLE_FROM, 32):
-        step("V", ("AD", banks[n][0], banks[n][1]), [("MU", banks[n][0], banks[n][1])])
-    for grp, m in order:
-        if grp == "v":
-            step("D", ("ST", grp, m), [("VC", grp, m)])
-        elif banks.index((grp, m)) >= SINGLE_FROM:
-            step("D", ("ST", grp, m), [("AD", grp, m), ("PA", grp, m)])
-        elif m % 2 == 1:
-            step("D", ("ST", grp, m), [("AD", grp, m), ("PA", grp, m - 1), ("PA", grp, m)])
+        lists["V"].append(("AD", BANKS[n][0], BANKS[n][1]))
+    stream = names(SCALAR_STREAM)
+    for j in range(len(stream)):
+        lists["S"].append(stream[j])
+        lists["S"].extend(copies[COPIES * j // STEPS:COPIES * (j + 1) // STEPS])
+    lists["S"].extend(copies[COPIES * len(stream) // STEPS:])
+    for name in lists["P"]:
+        if name[0] == "MM" and store_step(name[1], name[2]) == ("ST", name[1], name[2]):
+            lists["D"].append(("ST", name[1], name[2]))
+
+    needs = {}
+    for engine in ("D", "G", "P", "S", "V"):
+        for name in lists[engine]:
+            kind, grp, n = name
+            if kind in ("L", "const"):
+                before = []
+            elif kind in ("warm", "tab"):
+                before = [("const", ".", 0)]
+            elif kind == "sin":
+                before = [("tab", ".", 0)]
+            elif kind == "T":
+                before = [("L", "x", n), ("const", ".", 0)]
+            elif kind == "C":
+                before = [("T", "x", n)]
+            elif kind == "X":
+                before = [("C", "x", n - 1), ("C", "x", n)]
+            elif kind == "W":
+                before = [("L", "q0" if grp == "q0" else "qs", n), ("L", "sc", 0)]
+            elif kind == "I" and (grp, n) in TENSOR_INTERLEAVE:
+                before = [("J", grp, n)]
+            elif kind in ("I", "J"):
+                before = [("L", grp, n) if grp in ("k", "v") else ("W", grp, n)]
+            elif kind == "Q" and grp in ("q1", "q2"):
+                c = PASSES * ("q1", "q2").index(grp) + n
+                before = [("I", ("q1", "q2")[(c - 1) // PASSES], (c - 1) % PASSES), ("I", grp, n)]
+            elif kind == "Q":
+                before = [("I", grp, n)]
+            elif kind == "MM":
+                before = [quantise_step(grp, g) for g in range(PASSES)] + [("X", "x", (n // 2) | 1)]
+            elif kind == "MU":
+                before = [("MM", grp, n), ("sin", ".", 0)]
+            elif kind in ("PA", "VC"):
+                before = [("MM", grp, n)]
+            elif kind == "AD":
+                before = [("MU", grp, n)] if BANKS.index((grp, n)) >= SINGLE_FROM else [("MU", grp, n - 1), ("MU", grp, n)]
+            elif grp == "v":
+                before = [("VC", grp, n)]
+            else:
+                before = [("AD", grp, n), ("PA", grp, n)] + ([("PA", grp, n - 1)] if BANKS.index((grp, n)) < SINGLE_FROM else [])
+            needs[name] = before
 
     def ring(bufs, taken):
         for n in range(bufs, len(taken)):
             needs[taken[n][0]] = needs[taken[n][0]] + taken[n - bufs][1]
 
-    ring(WIDE_BUFS, [(s, [("I", s[1], s[2])]) for s in lists["S"] if s[0] == "W"])
-    ring(WG_BUFS, [(s, [("Q", s[1], s[2])]) for s in lists["V"] if s[0] == "I"])
-    ring(WG_PAIR_BUFS, [(s, [stream_quantise(s[1], s[2])]) for s in lists["S"] if s[0] == "I" and stream_quantise(s[1], s[2]) != ("Q", s[1], s[2])])
+    def reader(grp, g):
+        return ("J" if (grp, g) in TENSOR_INTERLEAVE else "I", grp, g)
+
+    ring(WIDE_BUFS, [(s, [reader(s[1], s[2])]) for s in lists["S"] if s[0] == "W"])
+    ring(RAW_BUFS, [(s, [reader(s[1], s[2])]) for s in lists["D"] if s[0] == "L" and s[1] in ("k", "v")])
+    ring(WG_BUFS, [(s, [quantise_step(s[1], s[2])]) for s in lists["V"] if s[0] == "I" and s[1] not in ("q1", "q2")])
+    ring(WG_LATE_BUFS, [(s, [quantise_step(s[1], s[2])]) for s in lists["S"] if s[0] == "I" and s[1] not in ("q1", "q2")])
     ring(XG_BUFS // PASSES, [(s, [("X", s[1], s[2] + 1)]) for s in lists["S"] if s[0] == "C" and s[2] % 2 == 0])
     ring(XZ_BUFS, [(s, [("T", "x", s[2])]) for s in lists["D"] if s[0] == "L" and s[1] == "x"]
-         + [(s, [("AD", s[1], s[2] + 1)]) for s in lists["V"] if s[0] == "MU" and s[2] % 2 == 0])
-    ring(O_BUFS, [(s, [("ST", s[1], s[2] + 1)]) for s in lists["P"] if s[0] == "MM" and s[1] != "v" and s[2] % 2 == 0])
-    ring(OV_BUFS, [(s, [("ST", s[1], s[2])]) for s in lists["P"] if s[0] == "MM" and s[1] == "v"])
+         + [(s, [add_step(s[1], s[2]), add_step(s[1], s[2] + 1)]) for s in lists["V"] if s[0] == "MU" and s[2] % 2 == 0])
+    ring(O_BUFS, [(s, [store_step(s[1], s[2]), store_step(s[1], s[2] + 1)]) for s in lists["P"] if s[0] == "MM" and s[1] != "v" and s[2] % 2 == 0])
+    ring(OV_BUFS, [(s, [store_step(s[1], s[2])]) for s in lists["P"] if s[0] == "MM" and s[1] == "v"])
     in_psum = []
     for s in lists["P"]:
         if s[0] == "T":
             in_psum.extend([(s, [("C", s[1], s[2])])] * PASSES)
+        elif s[0] == "J":
+            in_psum.extend([(s, [("I", s[1], s[2])])] * 2)
         elif s[1] == "v":
             in_psum.append((s, [("VC", s[1], s[2])]))
         else:
@@ -244,10 +232,6 @@ def tile_phi4miniattention_pa_kernel(tc, hidden_states, Wq_bytes, Wq_scale, Wk, 
             wq_bytes_sb[("q1", g)] = b2_t[:, :, 0:NB]
             wq_bytes_sb[("q2", g)] = b2_t[:, :, NB:2 * NB]
         planes = {}
-        for grp in ("k", "v"):
-            for g in range(PASSES):
-                r_t = keep.tile([P, 4, NB], BF16, name="raw%s%d" % (grp, g))
-                planes[(grp, g)] = r_t
         xc = []
         xs = []
         for g in range(PASSES):
@@ -272,13 +256,10 @@ def tile_phi4miniattention_pa_kernel(tc, hidden_states, Wq_bytes, Wq_scale, Wk, 
         warm = keep.tile([P, 1], F32, name="warm")
         pos = keep.tile([P, 4], F32, name="pos")
         ident = keep.tile([P, P], F32, name="ident")
-        theta = keep.tile([P, 4, HALF], F32, name="theta")
-        turns_i = keep.tile([P, 4, HALF], I32, name="turns_i")
-        turns = keep.tile([P, 4, HALF], F32, name="turns")
-        red = keep.tile([P, 4, HALF], F32, name="red")
+        theta = keep.tile([P, 2, 4, HALF], F32, name="theta")
+        turns = keep.tile([P, 2, 4, HALF], I32, name="turns")
+        red = keep.tile([P, 2, 4, HALF], F32, name="red")
         args = keep.tile([P, 2, 4, HALF], F32, name="args")
-        halfsin = keep.tile([P, 2, 4, HALF], F32, name="halfsin")
-        sq = keep.tile([P, 2, 4, HALF], F32, name="sq")
         rot = keep.tile([P, 4, 2, 2, HALF], F32, name="rot")
         live = {}
 
@@ -290,7 +271,9 @@ def tile_phi4miniattention_pa_kernel(tc, hidden_states, Wq_bytes, Wq_scale, Wk, 
                 x_sb[g] = x_t
                 nc.sync.dma_start(out=x_t[:], in_=hs[2 * P * g:2 * P * (g + 1), :].rearrange("(b p) k -> p b k", b=2))
             elif grp in ("k", "v"):
-                nc.sync.dma_start(out=planes[(grp, g)][:], in_=w_dram[grp][g])
+                raw = stage.tile([P, 4, NB], BF16, name="raw", tag="raw", bufs=RAW_BUFS)
+                planes[(grp, g)] = raw
+                nc.sync.dma_start(out=raw[:], in_=w_dram[grp][g])
             elif grp == "q0":
                 nc.sync.dma_start(out=wq_bytes_sb[(grp, g)], in_=wq_v[g][:, :, 0:NB])
             else:
@@ -302,24 +285,28 @@ def tile_phi4miniattention_pa_kernel(tc, hidden_states, Wq_bytes, Wq_scale, Wk, 
             make_identity(nc, ident[:])
 
         def table_angles():
-            nc.vector.tensor_copy(out=theta[:, :, 0:1], in_=pos[:].unsqueeze(2))
-            for s in (1, 2, 4, 8, 16):
-                nc.vector.tensor_scalar(out=theta[:, :, s:2 * s], in0=theta[:, :, 0:s], scalar1=BASE ** (-s / 48.0), scalar2=None, op0=ALU.mult)
-            nc.vector.tensor_scalar(out=theta[:, :, 32:48], in0=theta[:, :, 0:16], scalar1=BASE ** (-32 / 48.0), scalar2=None, op0=ALU.mult)
-            nc.vector.tensor_scalar(out=turns_i[:], in0=theta[:], scalar1=1.0 / (2.0 * math.pi), scalar2=None, op0=ALU.mult)
-            nc.vector.tensor_copy(out=turns[:], in_=turns_i[:])
+            for j in range(4):
+                nc.vector.tensor_scalar(out=theta[:, 0, :, j:j + 1], in0=pos[:].unsqueeze(2), scalar1=BASE ** (-j / 48.0), scalar2=None, op0=ALU.mult)
+            for j in (4, 8, 12):
+                nc.vector.tensor_scalar(out=theta[:, 0, :, j:j + 4], in0=theta[:, 0, :, 0:4], scalar1=BASE ** (-j / 48.0), scalar2=None, op0=ALU.mult)
+            for j in (16, 32):
+                nc.vector.tensor_scalar(out=theta[:, 0, :, j:j + 16], in0=theta[:, 0, :, 0:16], scalar1=BASE ** (-j / 48.0), scalar2=None, op0=ALU.mult)
+            nc.vector.tensor_scalar(out=theta[:, 1], in0=theta[:, 0], scalar1=0.5 * math.pi, scalar2=None, op0=ALU.add)
+            nc.vector.tensor_scalar(out=turns[:], in0=theta[:], scalar1=1.0 / (2.0 * math.pi), scalar2=None, op0=ALU.mult)
             c_hi = 6.28125
             c_lo = 2.0 * math.pi - c_hi
-            nc.vector.scalar_tensor_tensor(out=red[:], in0=turns[:], scalar=-c_hi, in1=theta[:], op0=ALU.mult, op1=ALU.add)
-            nc.vector.scalar_tensor_tensor(out=args[:, 0], in0=turns[:], scalar=-c_lo, in1=red[:], op0=ALU.mult, op1=ALU.add)
-            nc.vector.tensor_scalar(out=args[:, 1], in0=args[:, 0], scalar1=-0.5 * math.pi, scalar2=None, op0=ALU.add)
+            flat = "p a b j -> p (a b j)"
+            nc.vector.scalar_tensor_tensor(out=red[:].rearrange(flat), in0=turns[:].rearrange(flat), scalar=-c_hi, in1=theta[:].rearrange(flat), op0=ALU.mult, op1=ALU.add)
+            nc.vector.scalar_tensor_tensor(out=args[:].rearrange(flat), in0=turns[:].rearrange(flat), scalar=-c_lo, in1=red[:].rearrange(flat), op0=ALU.mult, op1=ALU.add)
 
         def table_factors():
-            nc.vector.tensor_tensor(out=sq[:], in0=halfsin[:], in1=halfsin[:], op=ALU.mult)
-            nc.vector.tensor_scalar(out=rot[:, :, 0, 0, :], in0=sq[:, 0], scalar1=-2.0, scalar2=1.0, op0=ALU.mult, op1=ALU.add)
-            nc.vector.tensor_scalar(out=rot[:, :, 1, 1, :], in0=sq[:, 0], scalar1=-2.0, scalar2=1.0, op0=ALU.mult, op1=ALU.add)
-            nc.vector.tensor_scalar(out=rot[:, :, 1, 0, :], in0=sq[:, 1], scalar1=-2.0, scalar2=1.0, op0=ALU.mult, op1=ALU.add)
-            nc.vector.tensor_scalar(out=rot[:, :, 0, 1, :], in0=sq[:, 1], scalar1=2.0, scalar2=-1.0, op0=ALU.mult, op1=ALU.add)
+            nc.scalar.activation(out=rot[:, :, 0, 1, :], in_=args[:, 0], func=ACT.Sin, scale=-1.0)
+            nc.scalar.activation(out=rot[:, :, 1, 0, :], in_=args[:, 0], func=ACT.Sin)
+            nc.scalar.activation(
+                out=rot[:].rearrange("p b r f j -> p b (r f) j")[:, :, 0:4:3, :],
+                in_=args[:, 1].unsqueeze(2).to_broadcast([P, 4, 2, HALF]),
+                func=ACT.Sin,
+            )
 
         def x_transposes(i):
             for g in range(PASSES):
@@ -358,17 +345,24 @@ def tile_phi4miniattention_pa_kernel(tc, hidden_states, Wq_bytes, Wq_scale, Wk, 
                 )
 
         def interleave(engine, grp, g):
+            if grp in ("q1", "q2"):
+                pair, place, name = pair_of(grp, g)
+                if ("wg2", pair) not in live:
+                    wg2 = stage.tile([P, 2, NB, 4], BF16, name="wg2", tag="wg2", bufs=WG_PAIR_BUFS, align_bytes=64)
+                    live[("wg2", pair)] = wg2
+                dst = live[("wg2", pair)][:, place]
+            else:
+                if engine == "V":
+                    wg = stage.tile([P, NB, 4], BF16, name="wg", tag="wg", bufs=WG_BUFS, align_bytes=64)
+                else:
+                    wg = stage.tile([P, NB, 4], BF16, name="wg_late", tag="wg_late", bufs=WG_LATE_BUFS, align_bytes=64)
+                live[("wg", grp, g)] = wg
+                dst = wg[:]
             src = planes[(grp, g)][:].rearrange("p t (c i) -> p c t i", i=4)
             if engine == "V":
-                wg = stage.tile([P, NB, 4], BF16, name="wg", tag="wg", bufs=WG_BUFS, align_bytes=64)
-                live[("wg", grp, g)] = wg
-                nc.vector.tensor_copy(out=wg[:].rearrange("p (c i) t -> p c t i", i=4), in_=src)
+                nc.vector.tensor_copy(out=dst.rearrange("p (c i) t -> p c t i", i=4), in_=src)
             else:
-                c = PASSES * ("q1", "q2").index(grp) + g
-                if c % 2 == 0:
-                    wg2 = stage.tile([P, 2, NB, 4], BF16, name="wg2", tag="wg2", bufs=WG_PAIR_BUFS, align_bytes=64)
-                    live[("wg2", c // 2)] = wg2
-                nc.scalar.copy(out=live[("wg2", c // 2)][:, c % 2].rearrange("p (c i) t -> p c t i", i=4), in_=src)
+                nc.scalar.copy(out=dst.rearrange("p (c i) t -> p c t i", i=4), in_=src)
 
         def quantise_two(grp, g):
             c = PASSES * ("q1", "q2").index(grp) + g
@@ -444,11 +438,9 @@ def tile_phi4miniattention_pa_kernel(tc, hidden_states, Wq_bytes, Wq_scale, Wk, 
                 constants()
             elif kind == "warm":
                 nc.scalar.activation(out=warm[:], in_=zero1[:], func=ACT.Sin)
-            elif kind == "tab1":
+            elif kind == "tab":
                 table_angles()
             elif kind == "sin":
-                nc.scalar.activation(out=halfsin[:], in_=args[:], func=ACT.Sin, scale=0.5)
-            elif kind == "tab2":
                 table_factors()
             elif kind == "T":
                 x_transposes(n)
@@ -470,13 +462,13 @@ def tile_phi4miniattention_pa_kernel(tc, hidden_states, Wq_bytes, Wq_scale, Wk, 
                 rope_multiply(grp, n)
             elif kind == "PA":
                 pass_through(grp, n)
-            elif kind == "AD" and ROPE_GROUPS.index(grp) * 8 + n >= SINGLE_FROM:
+            elif kind == "AD" and BANKS.index((grp, n)) >= SINGLE_FROM:
                 rope_add(engine, grp, n, n)
             elif kind == "AD":
                 rope_add(engine, grp, n, n - 1)
             elif kind == "VC":
                 nc.scalar.copy(out=live[("o", grp, n)][:, 0, :], in_=live[("acc", grp, n)][:])
-            elif grp == "v" or ROPE_GROUPS.index(grp) * 8 + n >= SINGLE_FROM:
+            elif grp == "v" or BANKS.index((grp, n)) >= SINGLE_FROM:
                 nc.sync.dma_start(out=outs[grp][P * n:P * (n + 1), :], in_=live[("o", grp, n)][:, n % 2 if grp != "v" else 0, :])
             else:
                 nc.sync.dma_start(out=outs[grp][P * (n - 1):P * (n + 1), :].rearrange("(b p) c -> p b c", b=2), in_=live[("o", grp, n)][:])

@@ -44,8 +44,9 @@ SCALAR_FIRST = "W q0 0,W q1 0,sin . 0,W q0 1,W q0 2,C x 0,C x 1,C x 2,C x 3"
 VECTOR_FIRST = "I k 0,Q k 0,I q0 0,I k 1,Q q0 0,I k 2,Q k 1,I q0 1,Q k 2,I q0 2,Q q0 1,I q1 0,Q q0 2,X x 1,I v 0,X x 3,Q v 0,I v 1"
 VECTOR_BETWEEN = {0: "Q v 1", 1: "Q v 2", 5: "I q1 2", 9: "Q q1 1", 11: "Q q2 0", 21: "Q q2 2"}
 SCALAR_STREAM = "W q1 1,I v 2,W q1 2,W q2 0,I q1 1,I q2 0,W q2 1,I q2 1,W q2 2,I q2 2"
-COPIES, STEPS = 5, 2
-V_AFTER = range(12, 28, 2)
+COPIES, STEPS = 7, 3
+BEHIND = 4
+V_AFTER = range(15, 31, 2)
 TENSOR_INTERLEAVE = ()
 
 
@@ -103,8 +104,8 @@ def engine_lists():
     stream = names(SCALAR_STREAM)
     for j in range(len(stream)):
         lists["S"].append(stream[j])
-        lists["S"].extend(copies[COPIES * j // STEPS:COPIES * (j + 1) // STEPS])
-    lists["S"].extend(copies[COPIES * len(stream) // STEPS:])
+        lists["S"].extend(copies[max(0, COPIES * j // STEPS - BEHIND):max(0, COPIES * (j + 1) // STEPS - BEHIND)])
+    lists["S"].extend(copies[COPIES * len(stream) // STEPS - BEHIND:])
     for name in lists["P"]:
         if name[0] == "MM" and store_step(name[1], name[2]) == ("ST", name[1], name[2]):
             lists["D"].append(("ST", name[1], name[2]))
@@ -140,8 +141,10 @@ def engine_lists():
                 before = [quantise_step(grp, g) for g in range(PASSES)] + [("X", "x", (n // 2) | 1)]
             elif kind == "MU":
                 before = [("MM", grp, n), ("sin", ".", 0)]
-            elif kind in ("PA", "VC"):
+            elif kind == "VC":
                 before = [("MM", grp, n)]
+            elif kind == "PA":
+                before = [("MU", grp, n)]
             elif kind == "AD":
                 before = [("MU", grp, n)] if BANKS.index((grp, n)) >= SINGLE_FROM else [("MU", grp, n - 1), ("MU", grp, n)]
             elif grp == "v":

@@ -28,6 +28,7 @@ FLOPS = 2 * TOKENS * K * 2560
 
 ROPE_GROUPS = ("k", "q0", "q1", "q2")
 SINGLE_FROM = 30
+VECTOR_ADDS = {20: 19, 30: 29}
 WIDE_BUFS = 4
 RAW_BUFS = 3
 WG_BUFS = 4
@@ -44,9 +45,9 @@ SCALAR_FIRST = "W q0 0,W q1 0,sin . 0,W q0 1,W q0 2,C x 0,C x 1,C x 2,C x 3"
 VECTOR_FIRST = "I k 0,Q k 0,I q0 0,I k 1,Q q0 0,I k 2,Q k 1,I q0 1,Q k 2,I q0 2,Q q0 1,I q1 0,Q q0 2,X x 1,I v 0,X x 3,Q v 0,I v 1"
 VECTOR_BETWEEN = {0: "Q v 1", 1: "Q v 2", 5: "I q1 2", 9: "Q q1 1", 11: "Q q2 0", 21: "Q q2 2"}
 SCALAR_STREAM = "W q1 1,I v 2,W q1 2,W q2 0,I q1 1,I q2 0,W q2 1,I q2 1,W q2 2,I q2 2"
-COPIES, STEPS = 7, 3
+PACE = 3
 BEHIND = 4
-V_AFTER = range(15, 31, 2)
+V_AFTER = range(10, 26, 2)
 TENSOR_INTERLEAVE = ()
 
 
@@ -97,15 +98,23 @@ def engine_lists():
         lists["V"].append(("MU", grp, m))
         if n in VECTOR_BETWEEN:
             lists["V"].extend(names(VECTOR_BETWEEN[n]))
-        if n < SINGLE_FROM and m % 2 == 1:
+        if n in VECTOR_ADDS:
+            lists["V"].append(("AD", BANKS[VECTOR_ADDS[n]][0], BANKS[VECTOR_ADDS[n]][1]))
+        if n < SINGLE_FROM and m % 2 == 1 and n not in VECTOR_ADDS.values():
             lists["G"].append(("AD", grp, m))
     for n in range(SINGLE_FROM, 32):
         lists["V"].append(("AD", BANKS[n][0], BANKS[n][1]))
     stream = names(SCALAR_STREAM)
+    beside = lists["V"][lists["V"].index(("MU", "k", 0)):]
+    done = 0
     for j in range(len(stream)):
         lists["S"].append(stream[j])
-        lists["S"].extend(copies[max(0, COPIES * j // STEPS - BEHIND):max(0, COPIES * (j + 1) // STEPS - BEHIND)])
-    lists["S"].extend(copies[COPIES * len(stream) // STEPS - BEHIND:])
+        for kind, grp, n in beside[max(0, PACE * j - BEHIND):max(0, PACE * (j + 1) - BEHIND)]:
+            if kind == "MU":
+                last = copies.index(("PA", grp, n)) + 1
+                lists["S"].extend(copies[done:last])
+                done = last
+    lists["S"].extend(copies[done:])
     for name in lists["P"]:
         if name[0] == "MM" and store_step(name[1], name[2]) == ("ST", name[1], name[2]):
             lists["D"].append(("ST", name[1], name[2]))

@@ -48,7 +48,8 @@ SCALAR_STREAM = "W q1 1,I v 2,W q1 2,W q2 0,I q1 1,I q2 0,W q2 1,I q2 1,W q2 2,I
 PACE = 3
 BEHIND = 4
 V_AFTER = range(10, 26, 2)
-TENSOR_INTERLEAVE = ()
+TENSOR_BETWEEN = {9: "J q2 0"}
+TENSOR_INTERLEAVE = (("q2", 0),)
 
 
 def names(text):
@@ -90,6 +91,8 @@ def engine_lists():
     for n in range(32):
         grp, m = BANKS[n]
         lists["P"].append(("MM", grp, m))
+        if n in TENSOR_BETWEEN:
+            lists["P"].extend(names(TENSOR_BETWEEN[n]))
         copies.append(("PA", grp, m))
         if n in V_AFTER:
             lists["P"].append(("MM", "v", v_banks))
@@ -268,6 +271,7 @@ def tile_phi4miniattention_pa_kernel(tc, hidden_states, Wq_bytes, Wq_scale, Wk, 
         warm = keep.tile([P, 1], F32, name="warm")
         pos = keep.tile([P, 4], F32, name="pos")
         ident = keep.tile([P, P], F32, name="ident")
+        ident16 = keep.tile([P, P], BF16, name="ident16")
         theta = keep.tile([P, 2, 4, HALF], F32, name="theta")
         turns = keep.tile([P, 2, 4, HALF], I32, name="turns")
         red = keep.tile([P, 2, 4, HALF], F32, name="red")
@@ -295,6 +299,7 @@ def tile_phi4miniattention_pa_kernel(tc, hidden_states, Wq_bytes, Wq_scale, Wk, 
             nc.gpsimd.memset(zero1[:], 0.0)
             nc.gpsimd.iota(pos[:], pattern=[[P, 4]], base=0, channel_multiplier=1, allow_small_or_imprecise_dtypes=True)
             make_identity(nc, ident[:])
+            nc.gpsimd.tensor_copy(out=ident16[:], in_=ident[:])
 
         def table_angles():
             for j in range(4):
@@ -356,6 +361,19 @@ def tile_phi4miniattention_pa_kernel(tc, hidden_states, Wq_bytes, Wq_scale, Wk, 
                     scale=sc[:, g, t:t + 1],
                 )
 
+        def interleave_on_tensor(grp, g):
+            for h in range(2):
+                jt = psum.tile([P, NB // 2, 4], BF16, name="jt", tag="bank")
+                live[("jt", grp, g, h)] = jt
+                for u in range(2):
+                    nc.tensor.matmul(
+                        jt[:, :, 2 * u:2 * u + 2].rearrange("p c t -> p t c"),
+                        lhsT=ident16[:],
+                        rhs=planes[(grp, g)][:, 2 * u:2 * u + 2, NB // 2 * h:NB // 2 * (h + 1)],
+                        start=True,
+                        stop=True,
+                    )
+
         def interleave(engine, grp, g):
             if grp in ("q1", "q2"):
                 pair, place, name = pair_of(grp, g)
@@ -370,6 +388,14 @@ def tile_phi4miniattention_pa_kernel(tc, hidden_states, Wq_bytes, Wq_scale, Wk, 
                     wg = stage.tile([P, NB, 4], BF16, name="wg_late", tag="wg_late", bufs=WG_LATE_BUFS, align_bytes=64)
                 live[("wg", grp, g)] = wg
                 dst = wg[:]
+            if (grp, g) in TENSOR_INTERLEAVE:
+                for h in range(2):
+                    half = dst[:, NB // 2 * h:NB // 2 * (h + 1), :]
+                    if engine == "V":
+                        nc.vector.tensor_copy(out=half, in_=live[("jt", grp, g, h)][:])
+                    else:
+                        nc.scalar.copy(out=half, in_=live[("jt", grp, g, h)][:])
+                return
             src = planes[(grp, g)][:].rearrange("p t (c i) -> p c t i", i=4)
             if engine == "V":
                 nc.vector.tensor_copy(out=dst.rearrange("p (c i) t -> p c t i", i=4), in_=src)
@@ -468,6 +494,8 @@ def tile_phi4miniattention_pa_kernel(tc, hidden_states, Wq_bytes, Wq_scale, Wk, 
                 quantise_two(grp, n)
             elif kind == "Q":
                 quantise(grp, n)
+            elif kind == "J":
+                interleave_on_tensor(grp, n)
             elif kind == "MM":
                 products(grp, n)
             elif kind == "MU":

import math
from contextlib import ExitStack

import concourse.mybir as mybir
from concourse.masks import make_identity

F32 = mybir.dt.float32
BF16 = mybir.dt.bfloat16
U8 = mybir.dt.uint8
U32 = mybir.dt.uint32
I32 = mybir.dt.int32
FP8 = mybir.dt.float8_e4m3fn
FP8X4 = mybir.dt.float8_e4m3fn_x4
ALU = mybir.AluOpType
ACT = mybir.ActivationFunctionType

P = 128
TOKENS = 1024
K = 1536
PASSES = 3
HD = 128
ROT = 96
HALF = 48
BASE = 10000.0
NB = 512

FLOPS = 2 * TOKENS * K * 2560

ROPE_GROUPS = ("k", "q0", "q1", "q2")
SINGLE_FROM = 30
VECTOR_ADDS = {20: 19, 30: 29}
WIDE_BUFS = 4
RAW_BUFS = 3
WG_BUFS = 4
WG_LATE_BUFS = 1
WG_PAIR_BUFS = 3
XG_BUFS = 6
XZ_BUFS = 4
O_BUFS = 6
OV_BUFS = 4

BANKS = [(grp, m) for grp in ROPE_GROUPS for m in range(8)]
LOADS = "L sc 0,L q0 0,L k 0,L qs 0,L q0 1,L k 1,L q0 2,L k 2,L x 0,L x 1,L x 2,L x 3,L v 0,L v 1,L qs 1,L v 2,L qs 2"
SCALAR_FIRST = "W q0 0,W q1 0,sin . 0,W q0 1,W q0 2,C x 0,C x 1,C x 2,C x 3"
VECTOR_FIRST = "I k 0,Q k 0,I q0 0,I k 1,Q q0 0,I k 2,Q k 1,I q0 1,Q k 2,I q0 2,Q q0 1,I q1 0,Q q0 2,X x 1,I v 0,X x 3,Q v 0,I v 1"
VECTOR_BETWEEN = {0: "Q v 1", 1: "Q v 2", 5: "I q1 2", 9: "Q q1 1", 11: "Q q2 0", 21: "Q q2 2"}
SCALAR_STREAM = "W q1 1,I v 2,W q1 2,W q2 0,I q1 1,I q2 0,W q2 1,I q2 1,W q2 2,I q2 2"
PACE = 3
BEHIND = 4
V_AFTER = range(10, 26, 2)
TENSOR_BETWEEN = {9: "J q2 0"}
TENSOR_INTERLEAVE = (("q2", 0),)


def names(text):
    out = []
    for word in text.split(","):
        kind, grp, n = word.split(" ")
        out.append((kind, grp, int(n)))
    return out


def pair_of(grp, g):
    c = PASSES * ("q1", "q2").index(grp) + g
    last = c | 1
    return c // 2, c % 2, ("Q", ("q1", "q2")[last // PASSES], last % PASSES)


def quantise_step(grp, g):
    if grp in ("q1", "q2"):
        return pair_of(grp, g)[2]
    return ("Q", grp, g)


def add_step(grp, m):
    if BANKS.index((grp, m)) >= SINGLE_FROM:
        return ("AD", grp, m)
    return ("AD", grp, m | 1)


def store_step(grp, m):
    if grp == "v" or BANKS.index((grp, m)) >= SINGLE_FROM:
        return ("ST", grp, m)
    return ("ST", grp, m | 1)


def engine_lists():
    lists = {"D": names(LOADS), "G": [("const", ".", 0)], "P": [("T", "x", i) for i in range(4)], "S": [("warm", ".", 0)] + names(SCALAR_FIRST), "V": [("tab", ".", 0)] + names(VECTOR_FIRST)}
    copies = []
    v_banks = 0
    for n in range(32):
        grp, m = BANKS[n]
        lists["P"].append(("MM", grp, m))
        if n in TENSOR_BETWEEN:
            lists["P"].extend(names(TENSOR_BETWEEN[n]))
        copies.append(("PA", grp, m))
        if n in V_AFTER:
            lists["P"].append(("MM", "v", v_banks))
            copies.append(("VC", "v", v_banks))
            v_banks += 1
        lists["V"].append(("MU", grp, m))
        if n in VECTOR_BETWEEN:
            lists["V"].extend(names(VECTOR_BETWEEN[n]))
        if n in VECTOR_ADDS:
            lists["V"].append(("AD", BANKS[VECTOR_ADDS[n]][0], BANKS[VECTOR_ADDS[n]][1]))
        if n < SINGLE_FROM and m % 2 == 1 and n not in VECTOR_ADDS.values():
            lists["G"].append(("AD", grp, m))
    for n in range(SINGLE_FROM, 32):
        lists["V"].append(("AD", BANKS[n][0], BANKS[n][1]))
    stream = names(SCALAR_STREAM)
    beside = lists["V"][lists["V"].index(("MU", "k", 0)):]
    done = 0
    for j in range(len(stream)):
        lists["S"].append(stream[j])
        for kind, grp, n in beside[max(0, PACE * j - BEHIND):max(0, PACE * (j + 1) - BEHIND)]:
            if kind == "MU":
                last = copies.index(("PA", grp, n)) + 1
                lists["S"].extend(copies[done:last])
                done = last
    lists["S"].extend(copies[done:])
    for name in lists["P"]:
        if name[0] == "MM" and store_step(name[1], name[2]) == ("ST", name[1], name[2]):
            lists["D"].append(("ST", name[1], name[2]))

    needs = {}
    for engine in ("D", "G", "P", "S", "V"):
        for name in lists[engine]:
            kind, grp, n = name
            if kind in ("L", "const"):
                before = []
            elif kind in ("warm", "tab"):
                before = [("const", ".", 0)]
            elif kind == "sin":
                before = [("tab", ".", 0)]
            elif kind == "T":
                before = [("L", "x", n), ("const", ".", 0)]
            elif kind == "C":
                before = [("T", "x", n)]
            elif kind == "X":
                before = [("C", "x", n - 1), ("C", "x", n)]
            elif kind == "W":
                before = [("L", "q0" if grp == "q0" else "qs", n), ("L", "sc", 0)]
            elif kind == "I" and (grp, n) in TENSOR_INTERLEAVE:
                before = [("J", grp, n)]
            elif kind in ("I", "J"):
                before = [("L", grp, n) if grp in ("k", "v") else ("W", grp, n)]
            elif kind == "Q" and grp in ("q1", "q2"):
                c = PASSES * ("q1", "q2").index(grp) + n
                before = [("I", ("q1", "q2")[(c - 1) // PASSES], (c - 1) % PASSES), ("I", grp, n)]
            elif kind == "Q":
                before = [("I", grp, n)]
            elif kind == "MM":
                before = [quantise_step(grp, g) for g in range(PASSES)] + [("X", "x", (n // 2) | 1)]
            elif kind == "MU":
                before = [("MM", grp, n), ("sin", ".", 0)]
            elif kind == "VC":
                before = [("MM", grp, n)]
            elif kind == "PA":
                before = [("MU", grp, n)]
            elif kind == "AD":
                before = [("MU", grp, n)] if BANKS.index((grp, n)) >= SINGLE_FROM else [("MU", grp, n - 1), ("MU", grp, n)]
            elif grp == "v":
                before = [("VC", grp, n)]
            else:
                before = [("AD", grp, n), ("PA", grp, n)] + ([("PA", grp, n - 1)] if BANKS.index((grp, n)) < SINGLE_FROM else [])
            needs[name] = before

    def ring(bufs, taken):
        for n in range(bufs, len(taken)):
            needs[taken[n][0]] = needs[taken[n][0]] + taken[n - bufs][1]

    def reader(grp, g):
        return ("J" if (grp, g) in TENSOR_INTERLEAVE else "I", grp, g)

    ring(WIDE_BUFS, [(s, [reader(s[1], s[2])]) for s in lists["S"] if s[0] == "W"])
    ring(RAW_BUFS, [(s, [reader(s[1], s[2])]) for s in lists["D"] if s[0] == "L" and s[1] in ("k", "v")])
    ring(WG_BUFS, [(s, [quantise_step(s[1], s[2])]) for s in lists["V"] if s[0] == "I" and s[1] not in ("q1", "q2")])
    ring(WG_LATE_BUFS, [(s, [quantise_step(s[1], s[2])]) for s in lists["S"] if s[0] == "I" and s[1] not in ("q1", "q2")])
    ring(XG_BUFS // PASSES, [(s, [("X", s[1], s[2] + 1)]) for s in lists["S"] if s[0] == "C" and s[2] % 2 == 0])
    ring(XZ_BUFS, [(s, [("T", "x", s[2])]) for s in lists["D"] if s[0] == "L" and s[1] == "x"]
         + [(s, [add_step(s[1], s[2]), add_step(s[1], s[2] + 1)]) for s in lists["V"] if s[0] == "MU" and s[2] % 2 == 0])
    ring(O_BUFS, [(s, [store_step(s[1], s[2]), store_step(s[1], s[2] + 1)]) for s in lists["P"] if s[0] == "MM" and s[1] != "v" and s[2] % 2 == 0])
    ring(OV_BUFS, [(s, [store_step(s[1], s[2])]) for s in lists["P"] if s[0] == "MM" and s[1] == "v"])
    in_psum = []
    for s in lists["P"]:
        if s[0] == "T":
            in_psum.extend([(s, [("C", s[1], s[2])])] * PASSES)
        elif s[0] == "J":
            in_psum.extend([(s, [("I", s[1], s[2])])] * 2)
        elif s[1] == "v":
            in_psum.append((s, [("VC", s[1], s[2])]))
        else:
            in_psum.append((s, [("MU", s[1], s[2]), ("PA", s[1], s[2])]))
    ring(8, in_psum)
    return lists, needs


def one_text(lists, needs):
    place = {"D": 0, "G": 0, "P": 0, "S": 0, "V": 0}
    written = set()
    text = []
    moved = True
    while moved:
        moved = False
        for engine in ("D", "G", "P", "S", "V"):
            while place[engine] < len(lists[engine]) and all(b in written for b in needs[lists[engine][place[engine]]]):
                name = lists[engine][place[engine]]
                text.append((engine, name))
                written.add(name)
                place[engine] += 1
                moved = True
    assert len(text) == sum(len(lists[engine]) for engine in ("D", "G", "P", "S", "V"))
    return text


def tile_phi4miniattention_pa_kernel(tc, hidden_states, Wq_bytes, Wq_scale, Wk, Wv, out_0, out_1, out_2):
    nc = tc.nc
    with ExitStack() as ctx:
        keep = ctx.enter_context(tc.tile_pool(name="keep", bufs=1))
        stage = ctx.enter_context(tc.tile_pool(name="stage", bufs=WIDE_BUFS))
        work = ctx.enter_context(tc.tile_pool(name="work", bufs=O_BUFS))
        psum = ctx.enter_context(tc.psum_pool(name="psum", bufs=8))
        ctx.enter_context(tc.manual_schedule())

        hs = hidden_states.rearrange("b s k -> (b s) k")
        wq_v = Wq_bytes.rearrange("(g p t) h d -> g p t (h d)", p=P, t=4)
        w_dram = {
            "k": Wk.rearrange("(g p t) h d -> g p t (h d)", p=P, t=4),
            "v": Wv.rearrange("(g p t) h d -> g p t (h d)", p=P, t=4),
        }
        outs = {
            "q0": out_0.rearrange("b s h d -> (b s) (h d)")[:, 0:NB],
            "q1": out_0.rearrange("b s h d -> (b s) (h d)")[:, NB:2 * NB],
            "q2": out_0.rearrange("b s h d -> (b s) (h d)")[:, 2 * NB:3 * NB],
            "k": out_1.rearrange("b s h d -> (b s) (h d)"),
            "v": out_2.rearrange("b s h d -> (b s) (h d)"),
        }

        sc = keep.tile([P, PASSES, 4], F32, name="sc")
        x_sb = {}
        wq_bytes_sb = {}
        for g in range(PASSES):
            b_t = keep.tile([P, 4, NB], U8, name="wqbytesq0_%d" % g)
            wq_bytes_sb[("q0", g)] = b_t[:]
            b2_t = keep.tile([P, 4, 2 * NB], U8, name="wqbytesqs_%d" % g)
            wq_bytes_sb[("qs", g)] = b2_t[:]
            wq_bytes_sb[("q1", g)] = b2_t[:, :, 0:NB]
            wq_bytes_sb[("q2", g)] = b2_t[:, :, NB:2 * NB]
        planes = {}
        xc = []
        xs = []
        for g in range(PASSES):
            xc_t = keep.tile([P, TOKENS], U32, name="xc%d" % g, align_bytes=64)
            xs_t = keep.tile([P, TOKENS], U8, name="xs%d" % g, align_bytes=64)
            xc.append(xc_t)
            xs.append(xs_t)
        wc = {}
        ws = {}
        for grp in ("k", "q0", "v"):
            wc_t = keep.tile([P, PASSES, NB], U32, name="wc_" + grp, align_bytes=64)
            ws_t = keep.tile([P, PASSES, NB], U8, name="ws_" + grp, align_bytes=64)
            wc[grp] = wc_t[:]
            ws[grp] = ws_t[:]
        wc_stream = keep.tile([P, 2 * PASSES, NB], U32, name="wc_stream", align_bytes=64)
        ws_stream = keep.tile([P, 2 * PASSES, NB], U8, name="ws_stream", align_bytes=64)
        for grp in ("q1", "q2"):
            first = PASSES * ("q1", "q2").index(grp)
            wc[grp] = wc_stream[:, first:first + PASSES, :]
            ws[grp] = ws_stream[:, first:first + PASSES, :]
        zero1 = keep.tile([P, 1], F32, name="zero1")
        warm = keep.tile([P, 1], F32, name="warm")
        pos = keep.tile([P, 4], F32, name="pos")
        ident = keep.tile([P, P], F32, name="ident")
        ident16 = keep.tile([P, P], BF16, name="ident16")
        theta = keep.tile([P, 2, 4, HALF], F32, name="theta")
        turns = keep.tile([P, 2, 4, HALF], I32, name="turns")
        red = keep.tile([P, 2, 4, HALF], F32, name="red")
        args = keep.tile([P, 2, 4, HALF], F32, name="args")
        rot = keep.tile([P, 4, 2, 2, HALF], F32, name="rot")
        live = {}

        def load(grp, g):
            if grp == "sc":
                nc.sync.dma_start(out=sc[:], in_=Wq_scale.rearrange("(g p t) a b -> p g (t a b)", p=P, t=4))
            elif grp == "x":
                x_t = work.tile([P, 2, K], BF16, name="x", tag="xz", bufs=XZ_BUFS)
                x_sb[g] = x_t
                nc.sync.dma_start(out=x_t[:], in_=hs[2 * P * g:2 * P * (g + 1), :].rearrange("(b p) k -> p b k", b=2))
            elif grp in ("k", "v"):
                raw = stage.tile([P, 4, NB], BF16, name="raw", tag="raw", bufs=RAW_BUFS)
                planes[(grp, g)] = raw
                nc.sync.dma_start(out=raw[:], in_=w_dram[grp][g])
            elif grp == "q0":
                nc.sync.dma_start(out=wq_bytes_sb[(grp, g)], in_=wq_v[g][:, :, 0:NB])
            else:
                nc.sync.dma_start(out=wq_bytes_sb[(grp, g)], in_=wq_v[g][:, :, NB:3 * NB])

        def constants():
            nc.gpsimd.memset(zero1[:], 0.0)
            nc.gpsimd.iota(pos[:], pattern=[[P, 4]], base=0, channel_multiplier=1, allow_small_or_imprecise_dtypes=True)
            make_identity(nc, ident[:])
            nc.gpsimd.tensor_copy(out=ident16[:], in_=ident[:])

        def table_angles():
            for j in range(4):
                nc.vector.tensor_scalar(out=theta[:, 0, :, j:j + 1], in0=pos[:].unsqueeze(2), scalar1=BASE ** (-j / 48.0), scalar2=None, op0=ALU.mult)
            for j in (4, 8, 12):
                nc.vector.tensor_scalar(out=theta[:, 0, :, j:j + 4], in0=theta[:, 0, :, 0:4], scalar1=BASE ** (-j / 48.0), scalar2=None, op0=ALU.mult)
            for j in (16, 32):
                nc.vector.tensor_scalar(out=theta[:, 0, :, j:j + 16], in0=theta[:, 0, :, 0:16], scalar1=BASE ** (-j / 48.0), scalar2=None, op0=ALU.mult)
            nc.vector.tensor_scalar(out=theta[:, 1], in0=theta[:, 0], scalar1=0.5 * math.pi, scalar2=None, op0=ALU.add)
            nc.vector.tensor_scalar(out=turns[:], in0=theta[:], scalar1=1.0 / (2.0 * math.pi), scalar2=None, op0=ALU.mult)
            c_hi = 6.28125
            c_lo = 2.0 * math.pi - c_hi
            flat = "p a b j -> p (a b j)"
            nc.vector.scalar_tensor_tensor(out=red[:].rearrange(flat), in0=turns[:].rearrange(flat), scalar=-c_hi, in1=theta[:].rearrange(flat), op0=ALU.mult, op1=ALU.add)
            nc.vector.scalar_tensor_tensor(out=args[:].rearrange(flat), in0=turns[:].rearrange(flat), scalar=-c_lo, in1=red[:].rearrange(flat), op0=ALU.mult, op1=ALU.add)

        def table_factors():
            nc.scalar.activation(out=rot[:, :, 0, 1, :], in_=args[:, 0], func=ACT.Sin, scale=-1.0)
            nc.scalar.activation(out=rot[:, :, 1, 0, :], in_=args[:, 0], func=ACT.Sin)
            nc.scalar.activation(
                out=rot[:].rearrange("p b r f j -> p b (r f) j")[:, :, 0:4:3, :],
                in_=args[:, 1].unsqueeze(2).to_broadcast([P, 4, 2, HALF]),
                func=ACT.Sin,
            )

        def x_transposes(i):
            for g in range(PASSES):
                xt = psum.tile([P, 2, 2, P], F32, name="xt", tag="bank")
                live[("xt", i, g)] = xt
                for c in range(2):
                    words = x_sb[i][:, c, :].bitcast(F32)
                    for u in range(2):
                        nc.tensor.transpose(xt[:, c, u, :], words[:, 256 * g + u:256 * (g + 1):2], ident[:])

        def x_copies(i):
            for g in range(PASSES):
                if i % 2 == 0:
                    xg = stage.tile([P, 2, 1024], BF16, name="xg", tag="xg", bufs=XG_BUFS, align_bytes=64)
                    live[("xg", i // 2, g)] = xg
                dst = live[("xg", i // 2, g)][:, i % 2, :].bitcast(F32).rearrange("p (c r u) -> p c r u", c=2, u=2)
                nc.scalar.copy(out=dst, in_=live[("xt", i, g)][:].rearrange("p c u r -> p c r u"))

        def x_quantise(i):
            for g in range(PASSES):
                nc.vector.quantize_mx(
                    out=xc[g][:, 256 * (i - 1):256 * (i + 1)].bitcast(FP8X4),
                    scales=xs[g][:, 256 * (i - 1):256 * (i + 1)],
                    in_=live[("xg", i // 2, g)][:].rearrange("p b c -> p (b c)"),
                )

        def widen(grp, g):
            wide = stage.tile([P, 4, NB], BF16, name="wide", tag="wide")
            planes[(grp, g)] = wide
            for t in range(4):
                nc.scalar.activation(
                    out=wide[:, t, :],
                    in_=wq_bytes_sb[(grp, g)][:, t, :].bitcast(FP8),
                    func=ACT.Copy,
                    scale=sc[:, g, t:t + 1],
                )

        def interleave_on_tensor(grp, g):
            for h in range(2):
                jt = psum.tile([P, NB // 2, 4], BF16, name="jt", tag="bank")
                live[("jt", grp, g, h)] = jt
                for u in range(2):
                    nc.tensor.matmul(
                        jt[:, :, 2 * u:2 * u + 2].rearrange("p c t -> p t c"),
                        lhsT=ident16[:],
                        rhs=planes[(grp, g)][:, 2 * u:2 * u + 2, NB // 2 * h:NB // 2 * (h + 1)],
                        start=True,
                        stop=True,
                    )

        def interleave(engine, grp, g):
            if grp in ("q1", "q2"):
                pair, place, name = pair_of(grp, g)
                if ("wg2", pair) not in live:
                    wg2 = stage.tile([P, 2, NB, 4], BF16, name="wg2", tag="wg2", bufs=WG_PAIR_BUFS, align_bytes=64)
                    live[("wg2", pair)] = wg2
                dst = live[("wg2", pair)][:, place]
            else:
                if engine == "V":
                    wg = stage.tile([P, NB, 4], BF16, name="wg", tag="wg", bufs=WG_BUFS, align_bytes=64)
                else:
                    wg = stage.tile([P, NB, 4], BF16, name="wg_late", tag="wg_late", bufs=WG_LATE_BUFS, align_bytes=64)
                live[("wg", grp, g)] = wg
                dst = wg[:]
            if (grp, g) in TENSOR_INTERLEAVE:
                for h in range(2):
                    half = dst[:, NB // 2 * h:NB // 2 * (h + 1), :]
                    if engine == "V":
                        nc.vector.tensor_copy(out=half, in_=live[("jt", grp, g, h)][:])
                    else:
                        nc.scalar.copy(out=half, in_=live[("jt", grp, g, h)][:])
                return
            src = planes[(grp, g)][:].rearrange("p t (c i) -> p c t i", i=4)
            if engine == "V":
                nc.vector.tensor_copy(out=dst.rearrange("p (c i) t -> p c t i", i=4), in_=src)
            else:
                nc.scalar.copy(out=dst.rearrange("p (c i) t -> p c t i", i=4), in_=src)

        def quantise_two(grp, g):
            c = PASSES * ("q1", "q2").index(grp) + g
            nc.vector.quantize_mx(
                out=wc_stream[:, c - 1:c + 1, :].rearrange("p g n -> p (g n)").bitcast(FP8X4),
                scales=ws_stream[:, c - 1:c + 1, :].rearrange("p g n -> p (g n)"),
                in_=live[("wg2", c // 2)][:].rearrange("p b n t -> p (b n t)"),
            )

        def quantise(grp, g):
            nc.vector.quantize_mx(
                out=wc[grp][:, g, :].bitcast(FP8X4),
                scales=ws[grp][:, g, :],
                in_=live[("wg", grp, g)][:].rearrange("p n t -> p (n t)"),
            )

        def products(grp, m):
            acc = psum.tile([P, NB], F32, name="acc", tag="bank")
            live[("acc", grp, m)] = acc
            if grp == "v":
                ov = work.tile([P, 1, NB], F32, name="ov", tag="ov", bufs=OV_BUFS)
                live[("o", grp, m)] = ov
            elif m % 2 == 0:
                o = work.tile([P, 2, NB], F32, name="o", tag="o")
                live[("o", grp, m)] = o
                live[("o", grp, m + 1)] = o
            for g in range(PASSES):
                nc.tensor.matmul_mx(
                    out=acc[:],
                    lhsT=xc[g][:, P * m:P * (m + 1)].bitcast(FP8X4),
                    lhsT_scale=xs[g][:, P * m:P * (m + 1)],
                    rhs=wc[grp][:, g, :].bitcast(FP8X4),
                    rhs_scale=ws[grp][:, g, :],
                    start=(g == 0),
                    stop=(g == PASSES - 1),
                )

        def rope_multiply(grp, m):
            y = live[("acc", grp, m)][:].rearrange("p (h d) -> p h d", h=4)
            if m % 2 == 0:
                z = work.tile([P, 2, 4, 2, ROT], F32, name="z", tag="xz", bufs=XZ_BUFS)
                live[("z", grp, m)] = z
                live[("z", grp, m + 1)] = z
            nc.vector.tensor_tensor(
                out=live[("z", grp, m)][:, m % 2],
                in0=y[:, :, 0:ROT].unsqueeze(2).to_broadcast([P, 4, 2, ROT]),
                in1=rot[:, m % 4].rearrange("p r f j -> p r (f j)").unsqueeze(1).to_broadcast([P, 4, 2, ROT]),
                op=ALU.mult,
            )

        def pass_through(grp, m):
            y = live[("acc", grp, m)][:].rearrange("p (h d) -> p h d", h=4)
            oh = live[("o", grp, m)][:, m % 2, :].rearrange("p (h d) -> p h d", h=4)
            nc.scalar.copy(out=oh[:, :, ROT:HD], in_=y[:, :, ROT:HD])

        def rope_add(engine, grp, m, first):
            oh = live[("o", grp, m)][:, first % 2:m % 2 + 1, :].rearrange("p b (h d) -> p (b h) d", h=4)
            zv = live[("z", grp, m)][:, first % 2:m % 2 + 1].rearrange("p b h r (f j) -> p (b h) r f j", f=2)
            adder = nc.vector if engine == "V" else nc.gpsimd
            adder.tensor_tensor(
                out=oh[:, :, 0:ROT].rearrange("p h (r j) -> p h r j", r=2),
                in0=zv[:, :, :, 0, :],
                in1=zv[:, :, :, 1, :],
                op=ALU.add,
            )

        lists, needs = engine_lists()
        for engine, name in one_text(lists, needs):
            kind, grp, n = name
            if kind == "L":
                load(grp, n)
            elif kind == "const":
                constants()
            elif kind == "warm":
                nc.scalar.activation(out=warm[:], in_=zero1[:], func=ACT.Sin)
            elif kind == "tab":
                table_angles()
            elif kind == "sin":
                table_factors()
            elif kind == "T":
                x_transposes(n)
            elif kind == "C":
                x_copies(n)
            elif kind == "X":
                x_quantise(n)
            elif kind == "W":
                widen(grp, n)
            elif kind == "I":
                interleave(engine, grp, n)
            elif kind == "Q" and grp in ("q1", "q2"):
                quantise_two(grp, n)
            elif kind == "Q":
                quantise(grp, n)
            elif kind == "J":
                interleave_on_tensor(grp, n)
            elif kind == "MM":
                products(grp, n)
            elif kind == "MU":
                rope_multiply(grp, n)
            elif kind == "PA":
                pass_through(grp, n)
            elif kind == "AD" and BANKS.index((grp, n)) >= SINGLE_FROM:
                rope_add(engine, grp, n, n)
            elif kind == "AD":
                rope_add(engine, grp, n, n - 1)
            elif kind == "VC":
                nc.scalar.copy(out=live[("o", grp, n)][:, 0, :], in_=live[("acc", grp, n)][:])
            elif grp == "v" or BANKS.index((grp, n)) >= SINGLE_FROM:
                nc.sync.dma_start(out=outs[grp][P * n:P * (n + 1), :], in_=live[("o", grp, n)][:, n % 2 if grp != "v" else 0, :])
            else:
                nc.sync.dma_start(out=outs[grp][P * (n - 1):P * (n + 1), :].rearrange("(b p) c -> p b c", b=2), in_=live[("o", grp, n)][:])
